import numpy as np
import ml_dtypes


def mxq(x, axis, fmt="e4m3"):
    dtype, down = {"e4m3": (ml_dtypes.float8_e4m3fn, 7), "e5m2": (ml_dtypes.float8_e5m2, 14)}[fmt]
    v = np.moveaxis(np.asarray(x, np.float32).astype(ml_dtypes.bfloat16).astype(np.float64), axis, -1)
    blocks = v.reshape(v.shape[:-1] + (-1, 32))
    amax = np.abs(blocks).max(-1, keepdims=True)
    byte = np.maximum(np.where(amax > 0, np.frexp(amax)[1] - 1 + 127, 0) - down, 1)
    scale = np.exp2(byte - 127.0)
    codes = (blocks / scale).astype(np.float32).astype(dtype).astype(np.float64)
    return np.moveaxis((codes * scale).reshape(v.shape), -1, axis)


WIDE = False


def mx_kscale(k):
    if not WIDE:
        return np.ones(k)
    levels = np.array([10, -10, 5, -5, 0])
    if k % 512:
        return np.exp2(np.random.permutation(np.resize(levels, k // 32))).repeat(32)
    a = np.empty((k // 512, 16))
    for p in range(k // 512):
        a[p, :8] = np.random.permutation(np.resize(levels, 8))
        for g in range(8):
            far = levels[np.abs(levels - a[p, g]) >= 10]
            a[p, g + 8] = far[np.random.randint(len(far))]
    return np.exp2(a.ravel()).repeat(32)


BF16 = ml_dtypes.bfloat16


def bf(x):
    return np.asarray(x, np.float32).astype(BF16)


def f64(x):
    return np.asarray(x).astype(np.float64)


B, LC, LL, LLAMA_DIM, DIM, HEADS, FF = 16, 77, 256, 512, 512, 16, 6144
EPS = 1e-5


def layernorm(x, g, b):
    m = x.mean(-1, keepdims=True)
    v = ((x - m) ** 2).mean(-1, keepdims=True)
    return (x - m) / np.sqrt(v + EPS) * g + b


def setup_inputs():
    s, t = mx_kscale(LLAMA_DIM), mx_kscale(DIM)
    return {
        "llm_embed": bf(np.random.standard_normal((B, LL, LLAMA_DIM)) * s),
        "llm_proj_w": bf(np.random.standard_normal((DIM, LLAMA_DIM)) / np.sqrt(LLAMA_DIM) / s),
        "llm_proj_b": bf(0.1 * np.random.standard_normal(DIM)),
        "kvn_g": bf((1.0 + 0.1 * np.random.standard_normal(DIM)) * t),
        "kvn_b": bf(0.1 * np.random.standard_normal(DIM) * t),
        "q_w": bf(np.random.standard_normal((DIM, DIM)) / np.sqrt(DIM) / t),
        "q_b": bf(0.1 * np.random.standard_normal(DIM)),
    }


def reference(llm_embed, llm_proj_w, llm_proj_b, kvn_g, kvn_b, q_w, q_b):
    llm = (mxq(f64(llm_embed), 2, "e4m3") @ mxq(f64(llm_proj_w), 1, "e4m3").T) + f64(llm_proj_b)
    llm_n = layernorm(llm, f64(kvn_g), f64(kvn_b))
    q = (mxq(llm_n, 2, "e4m3") @ mxq(f64(q_w), 1, "e4m3").T) + f64(q_b)
    return llm, q

@@ -1,0 +1,296 @@
+from contextlib import ExitStack
+
+import concourse.mybir as mybir
+from concourse.masks import make_identity
+
+F32 = mybir.dt.float32
+BF16 = mybir.dt.bfloat16
+U32 = mybir.dt.uint32
+U8 = mybir.dt.uint8
+FP8X4 = mybir.dt.float8_e4m3fn_x4
+ACT = mybir.ActivationFunctionType
+ALU = mybir.AluOpType
+
+P = 128
+PACK = 4
+D = P * PACK
+TOKENS = 16 * 256
+TILES = 2
+GROUP = P * TILES
+GROUPS = TOKENS // GROUP
+RUN = 8
+EPS = 1e-5
+LAST_LAG = 7
+W2_TRANSPOSE_STEP = 3
+W2_QUANTISE_STEP = 4
+
+FLOPS = 2 * 2 * TOKENS * D * D
+
+
+def tile_crossfusion_pa_t_kernel(tc, x, w1, b1, gamma, beta, w2, b2, llm_out, q_out):
+    nc = tc.nc
+    x_groups = x.flatten_outer_dims().rearrange("(g p j) k -> g p j k", p=P, j=TILES)
+    llm_groups = llm_out.flatten_outer_dims().rearrange("(g p j) f -> g p j f", p=P, j=TILES)
+    q_groups = q_out.flatten_outer_dims().rearrange("(g p j) f -> g p j f", p=P, j=TILES)
+
+    with ExitStack() as stack:
+        stack.enter_context(tc.manual_schedule())
+        const = stack.enter_context(tc.tile_pool(name="const", bufs=1))
+        x_pool = stack.enter_context(tc.tile_pool(name="x_pool", bufs=GROUPS))
+        work = stack.enter_context(tc.tile_pool(name="work", bufs=3))
+        wide = stack.enter_context(tc.tile_pool(name="wide", bufs=5))
+        small = stack.enter_context(tc.tile_pool(name="small", bufs=4))
+        psum_t = stack.enter_context(tc.psum_pool(name="psum_t", bufs=2))
+        psum_acc = stack.enter_context(tc.psum_pool(name="psum_acc", bufs=4))
+        psum_z = stack.enter_context(tc.psum_pool(name="psum_z", bufs=2))
+
+        x_sb = []
+        for g in range(GROUPS):
+            x_sb.append(x_pool.tile([P, TILES, D], BF16, name="x_sb", tag="x_sb"))
+        w1_sb = const.tile([P, PACK, D], BF16)
+        w2_sb = const.tile([P, PACK, D], BF16)
+        bias_rows = const.tile([P, 2, D], BF16)
+        param_rows = const.tile([P, P], BF16)
+        nc.vector.memset(bias_rows[:], 0.0)
+        nc.vector.memset(param_rows[:], 0.0)
+        nc.sync.dma_start(out=w1_sb[:], in_=w1.rearrange("(ob p) k -> p ob k", p=P))
+        nc.sync.dma_start(out=x_sb[0][:], in_=x_groups[0])
+        nc.sync.dma_start(out=bias_rows[0:1, 0, :], in_=b1.rearrange("(o f) -> o f", o=1))
+        nc.sync.dma_start(out=x_sb[1][:], in_=x_groups[1])
+        nc.sync.dma_start(out=x_sb[2][:], in_=x_groups[2])
+        nc.sync.dma_start(out=w2_sb[:], in_=w2.rearrange("(ob p) k -> p ob k", p=P))
+        nc.sync.dma_start(out=bias_rows[0:1, 1, :], in_=b2.rearrange("(o f) -> o f", o=1))
+        for n, vec in enumerate((gamma, beta)):
+            nc.sync.dma_start(
+                out=param_rows[n * PACK : (n + 1) * PACK, :].rearrange("t (s i) -> t s i", i=RUN),
+                in_=vec.rearrange("(s t i) -> t s i", t=PACK, i=RUN),
+            )
+        for g in range(3, GROUPS):
+            nc.sync.dma_start(out=x_sb[g][:], in_=x_groups[g])
+
+        ident_f32 = const.tile([P, P], F32)
+        make_identity(nc, ident_f32[:])
+        ident_bf = const.tile([P, P], BF16)
+        make_identity(nc, ident_bf[:])
+        ones = const.tile([P, P], BF16)
+        nc.vector.memset(ones[:], 1.0)
+        warm = const.tile([P, 1], F32)
+        nc.vector.memset(warm[:], 1.0)
+        nc.scalar.sqrt(out=warm[:], in_=warm[:])
+
+        def word_transposes(rows, grouped, on_vector):
+            words = rows.bitcast(F32)
+            planes_ps = psum_t.tile([P, 2, 2 * P], F32, name="planes_ps", tag="tp")
+            for b in range(2):
+                for u in range(2):
+                    nc.tensor.transpose(
+                        planes_ps[:, u, b * P : (b + 1) * P], words[:, b, u : 2 * P : 2], ident_f32[:]
+                    )
+            if on_vector:
+                nc.vector.tensor_copy(out=grouped.bitcast(F32), in_=planes_ps[:].rearrange("p u c -> p c u"))
+            else:
+                nc.scalar.copy(out=grouped.bitcast(F32), in_=planes_ps[:].rearrange("p u c -> p c u"))
+
+        def quantise(grouped, codes, scales):
+            nc.vector.quantize_mx(
+                out=codes.bitcast(FP8X4),
+                scales=scales,
+                in_=grouped.rearrange("p c t -> p (c t)"),
+            )
+
+        w1_grouped = const.tile([P, D, PACK], BF16, align_bytes=64)
+        w1_codes = const.tile([P, D], U32, align_bytes=64)
+        w1_scales = const.tile([P, D], U8, align_bytes=64)
+        word_transposes(w1_sb[:, 0:2, :], w1_grouped[:, 0 : 2 * P, :], True)
+        word_transposes(w1_sb[:, 2:4, :], w1_grouped[:, 2 * P : 4 * P, :], False)
+        quantise(w1_grouped[:], w1_codes[:], w1_scales[:])
+
+        bias_bc = const.tile([P, 2, D], F32)
+        params = const.tile([P, 2 * PACK], F32)
+        w2_grouped = const.tile([P, D, PACK], BF16, align_bytes=64)
+        w2_codes = const.tile([P, D], U32, align_bytes=64)
+        w2_scales = const.tile([P, D], U8, align_bytes=64)
+
+        w2_turned = const.tile([P, PACK, D], BF16)
+
+        def turn(features):
+            return features.rearrange("p (s t i) -> p t s i", t=PACK, i=RUN)
+
+        def unturned(features):
+            return features.rearrange("p (t s i) -> p t s i", t=PACK, i=RUN)
+
+        def turn_w2():
+            for b in range(PACK):
+                nc.gpsimd.tensor_scalar(
+                    out=unturned(w2_turned[:, b, :]),
+                    in0=turn(w2_sb[:, b, :]),
+                    scalar1=1.0,
+                    scalar2=0.0,
+                    op0=ALU.mult,
+                    op1=ALU.add,
+                )
+
+        def spread_bias(i):
+            bias_ps = psum_acc.tile([P, D], F32, name="bias_ps", tag="acc")
+            nc.tensor.matmul(bias_ps[:], lhsT=ones[:], rhs=bias_rows[:, i, :], start=True, stop=True)
+            nc.vector.tensor_copy(out=bias_bc[:, i, :], in_=bias_ps[:])
+
+        def w2_to_partitions():
+            param_ps = psum_t.tile([P, P], BF16, name="param_ps", tag="tp")
+            nc.tensor.transpose(param_ps[:], param_rows[:], ident_bf[:])
+            nc.scalar.copy(out=params[:], in_=param_ps[:, 0 : 2 * PACK])
+            for h in range(2):
+                w2_ps = psum_t.tile([P, PACK, 2 * P], BF16, name="w2_ps", tag="tp")
+                for b in range(2):
+                    for t in range(PACK):
+                        nc.tensor.transpose(
+                            w2_ps[:, t, b * P : (b + 1) * P],
+                            w2_turned[:, 2 * h + b, t * P : (t + 1) * P],
+                            ident_bf[:],
+                        )
+                nc.scalar.copy(
+                    out=w2_grouped[:, 2 * h * P : 2 * (h + 1) * P, :],
+                    in_=w2_ps[:].rearrange("p t c -> p c t"),
+                )
+
+        x_grouped, x_codes, x_scales = {}, {}, {}
+        llm, sums, neg_mean, std, z = {}, {}, {}, {}, {}
+        planes, n_grouped, n_codes, n_scales = {}, {}, {}, {}
+
+        def x_to_partitions(g):
+            x_grouped[g] = work.tile([P, GROUP, PACK], BF16, name="x_grouped", align_bytes=64)
+            word_transposes(x_sb[g][:], x_grouped[g][:], False)
+
+        def quantise_x(g):
+            x_codes[g] = work.tile([P, GROUP], U32, name="x_codes", align_bytes=64)
+            x_scales[g] = work.tile([P, GROUP], U8, name="x_scales", align_bytes=64)
+            quantise(x_grouped[g][:], x_codes[g][:], x_scales[g][:])
+
+        def first_matmul(g):
+            llm[g] = wide.tile([P, TILES, D], F32, name="llm")
+            sums[g] = small.tile([P, TILES], F32, name="sums")
+            for j in range(TILES):
+                cols = slice(j * P, (j + 1) * P)
+                acc = psum_acc.tile([P, D], F32, name="acc", tag="acc")
+                nc.tensor.matmul_mx(
+                    out=acc[:],
+                    lhsT=x_codes[g][:, cols].bitcast(FP8X4),
+                    lhsT_scale=x_scales[g][:, cols],
+                    rhs=w1_codes[:].bitcast(FP8X4),
+                    rhs_scale=w1_scales[:],
+                    start=True,
+                    stop=True,
+                )
+                nc.vector.scalar_tensor_tensor(
+                    out=llm[g][:, j, :],
+                    in0=acc[:],
+                    scalar=1.0,
+                    in1=bias_bc[:, 0, :],
+                    op0=ALU.mult,
+                    op1=ALU.add,
+                    accum_out=sums[g][:, j : j + 1],
+                )
+            nc.sync.dma_start(out=llm_groups[g], in_=llm[g][:])
+
+        def statistics(g):
+            neg_mean[g] = small.tile([P, TILES], F32, name="neg_mean")
+            nc.scalar.mul(out=neg_mean[g][:], in_=sums[g][:], mul=-1.0 / D)
+            squares = work.tile([P, TILES, D], BF16)
+            sum_sq = small.tile([P, TILES], F32)
+            for j in range(TILES):
+                nc.scalar.activation(
+                    out=squares[:, j, :],
+                    in_=llm[g][:, j, :],
+                    func=ACT.Square,
+                    bias=neg_mean[g][:, j : j + 1],
+                    scale=1.0,
+                    accum_out=sum_sq[:, j : j + 1],
+                )
+            std[g] = small.tile([P, TILES], F32, name="std")
+            nc.scalar.activation(out=std[g][:], in_=sum_sq[:], func=ACT.Sqrt, bias=EPS, scale=1.0 / D)
+
+        def normalise(g):
+            rstd = small.tile([P, TILES], F32)
+            nc.vector.reciprocal(out=rstd[:], in_=std[g][:])
+            z[g] = work.tile([P, TILES, D], F32, name="z")
+            for j in range(TILES):
+                nc.gpsimd.tensor_scalar(
+                    out=unturned(z[g][:, j, :]),
+                    in0=turn(llm[g][:, j, :]),
+                    scalar1=neg_mean[g][:, j : j + 1],
+                    scalar2=rstd[:, j : j + 1],
+                    op0=ALU.add,
+                    op1=ALU.mult,
+                )
+
+        def features_to_partitions(g):
+            planes[g] = work.tile([P, PACK, GROUP], BF16, name="planes")
+            for h in range(2):
+                z_ps = psum_z.tile([P, 2, GROUP], F32, name="z_ps", tag="z_ps")
+                for i in range(2):
+                    t = 2 * h + i
+                    for j in range(TILES):
+                        nc.tensor.transpose(
+                            z_ps[:, i, j * P : (j + 1) * P], z[g][:, j, t * P : (t + 1) * P], ident_f32[:]
+                        )
+                for i in range(2):
+                    t = 2 * h + i
+                    nc.scalar.activation(
+                        out=planes[g][:, t, :],
+                        in_=z_ps[:, i, :],
+                        func=ACT.Identity,
+                        bias=params[:, PACK + t : PACK + t + 1],
+                        scale=params[:, t : t + 1],
+                    )
+
+        def regroup_n(g):
+            n_grouped[g] = work.tile([P, GROUP, PACK], BF16, name="n_grouped", align_bytes=64)
+            nc.vector.tensor_copy(
+                out=n_grouped[g][:].rearrange("p (c i) t -> p c t i", i=4),
+                in_=planes[g][:].rearrange("p t (c i) -> p c t i", i=4),
+            )
+
+        def quantise_n(g):
+            n_codes[g] = work.tile([P, GROUP], U32, name="n_codes", align_bytes=64)
+            n_scales[g] = work.tile([P, GROUP], U8, name="n_scales", align_bytes=64)
+            quantise(n_grouped[g][:], n_codes[g][:], n_scales[g][:])
+
+        def second_matmul(g):
+            q = wide.tile([P, TILES, D], F32)
+            for j in range(TILES):
+                cols = slice(j * P, (j + 1) * P)
+                acc = psum_acc.tile([P, D], F32, name="acc", tag="acc")
+                nc.tensor.matmul_mx(
+                    out=acc[:],
+                    lhsT=n_codes[g][:, cols].bitcast(FP8X4),
+                    lhsT_scale=n_scales[g][:, cols],
+                    rhs=w2_codes[:].bitcast(FP8X4),
+                    rhs_scale=w2_scales[:],
+                    start=True,
+                    stop=True,
+                )
+                nc.vector.tensor_add(out=q[:, j, :], in0=acc[:], in1=bias_bc[:, 1, :])
+                nc.sync.dma_start(out=q_groups[g][:, j, :], in_=q[:, j, :])
+
+        def run(stage, g):
+            if 0 <= g < GROUPS:
+                stage(g)
+
+        for step in range(GROUPS + LAST_LAG):
+            run(x_to_partitions, step)
+            run(regroup_n, step - 6)
+            run(quantise_x, step - 1)
+            run(quantise_n, step - 6)
+            run(normalise, step - 4)
+            run(first_matmul, step - 2)
+            run(second_matmul, step - 7)
+            run(statistics, step - 3)
+            run(features_to_partitions, step - 5)
+            if step == 0:
+                spread_bias(0)
+                turn_w2()
+            if step == W2_TRANSPOSE_STEP:
+                w2_to_partitions()
+            if step == W2_QUANTISE_STEP:
+                quantise(w2_grouped[:], w2_codes[:], w2_scales[:])
+                spread_bias(1)

@@ -20,9 +20,6 @@ GROUP = P * TILES
 GROUPS = TOKENS // GROUP
 RUN = 8
 EPS = 1e-5
-LAST_LAG = 7
-W2_TRANSPOSE_STEP = 3
-W2_QUANTISE_STEP = 4
 
 FLOPS = 2 * 2 * TOKENS * D * D
 
@@ -78,18 +75,15 @@ def tile_crossfusion_pa_t_kernel(tc, x, w1, b1, gamma, beta, w2, b2, llm_out, q_
         nc.vector.memset(warm[:], 1.0)
         nc.scalar.sqrt(out=warm[:], in_=warm[:])
 
-        def word_transposes(rows, grouped, on_vector):
+        def word_transposes(rows):
             words = rows.bitcast(F32)
-            planes_ps = psum_t.tile([P, 2, 2 * P], F32, name="planes_ps", tag="tp")
+            words_ps = psum_t.tile([P, 2, 2 * P], F32, name="words_ps", tag="tp")
             for b in range(2):
                 for u in range(2):
                     nc.tensor.transpose(
-                        planes_ps[:, u, b * P : (b + 1) * P], words[:, b, u : 2 * P : 2], ident_f32[:]
+                        words_ps[:, u, b * P : (b + 1) * P], words[:, b, u : 2 * P : 2], ident_f32[:]
                     )
-            if on_vector:
-                nc.vector.tensor_copy(out=grouped.bitcast(F32), in_=planes_ps[:].rearrange("p u c -> p c u"))
-            else:
-                nc.scalar.copy(out=grouped.bitcast(F32), in_=planes_ps[:].rearrange("p u c -> p c u"))
+            return words_ps[:].rearrange("p u c -> p c u")
 
         def quantise(grouped, codes, scales):
             nc.vector.quantize_mx(
@@ -98,26 +92,29 @@ def tile_crossfusion_pa_t_kernel(tc, x, w1, b1, gamma, beta, w2, b2, llm_out, q_
                 in_=grouped.rearrange("p c t -> p (c t)"),
             )
 
-        w1_grouped = const.tile([P, D, PACK], BF16, align_bytes=64)
-        w1_codes = const.tile([P, D], U32, align_bytes=64)
-        w1_scales = const.tile([P, D], U8, align_bytes=64)
-        word_transposes(w1_sb[:, 0:2, :], w1_grouped[:, 0 : 2 * P, :], True)
-        word_transposes(w1_sb[:, 2:4, :], w1_grouped[:, 2 * P : 4 * P, :], False)
-        quantise(w1_grouped[:], w1_codes[:], w1_scales[:])
-
-        bias_bc = const.tile([P, 2, D], F32)
-        params = const.tile([P, 2 * PACK], F32)
-        w2_grouped = const.tile([P, D, PACK], BF16, align_bytes=64)
-        w2_codes = const.tile([P, D], U32, align_bytes=64)
-        w2_scales = const.tile([P, D], U8, align_bytes=64)
-
-        w2_turned = const.tile([P, PACK, D], BF16)
-
         def turn(features):
             return features.rearrange("p (s t i) -> p t s i", t=PACK, i=RUN)
 
         def unturned(features):
             return features.rearrange("p (t s i) -> p t s i", t=PACK, i=RUN)
+
+        w1_grouped = const.tile([P, D, PACK], BF16, align_bytes=64)
+        w1_codes = const.tile([P, D], U32, align_bytes=64)
+        w1_scales = const.tile([P, D], U8, align_bytes=64)
+        nc.vector.tensor_copy(
+            out=w1_grouped[:, 0 : 2 * P, :].bitcast(F32), in_=word_transposes(w1_sb[:, 0:2, :])
+        )
+        nc.scalar.copy(
+            out=w1_grouped[:, 2 * P : 4 * P, :].bitcast(F32), in_=word_transposes(w1_sb[:, 2:4, :])
+        )
+        quantise(w1_grouped[:], w1_codes[:], w1_scales[:])
+
+        bias_bc = const.tile([P, 2, D], F32)
+        params = const.tile([P, 2 * PACK], F32)
+        w2_turned = const.tile([P, PACK, D], BF16)
+        w2_grouped = const.tile([P, D, PACK], BF16, align_bytes=64)
+        w2_codes = const.tile([P, D], U32, align_bytes=64)
+        w2_scales = const.tile([P, D], U8, align_bytes=64)
 
         def turn_w2():
             for b in range(PACK):
@@ -135,12 +132,14 @@ def tile_crossfusion_pa_t_kernel(tc, x, w1, b1, gamma, beta, w2, b2, llm_out, q_
             nc.tensor.matmul(bias_ps[:], lhsT=ones[:], rhs=bias_rows[:, i, :], start=True, stop=True)
             nc.vector.tensor_copy(out=bias_bc[:, i, :], in_=bias_ps[:])
 
-        def w2_to_partitions():
+        def params_to_partitions():
             param_ps = psum_t.tile([P, P], BF16, name="param_ps", tag="tp")
             nc.tensor.transpose(param_ps[:], param_rows[:], ident_bf[:])
             nc.scalar.copy(out=params[:], in_=param_ps[:, 0 : 2 * PACK])
+
+        def w2_to_partitions():
             for h in range(2):
-                w2_ps = psum_t.tile([P, PACK, 2 * P], BF16, name="w2_ps", tag="tp")
+                w2_ps = psum_z.tile([P, PACK, 2 * P], BF16, name="w2_ps", tag="z_ps")
                 for b in range(2):
                     for t in range(PACK):
                         nc.tensor.transpose(
@@ -153,37 +152,49 @@ def tile_crossfusion_pa_t_kernel(tc, x, w1, b1, gamma, beta, w2, b2, llm_out, q_
                     in_=w2_ps[:].rearrange("p t c -> p c t"),
                 )
 
-        x_grouped, x_codes, x_scales = {}, {}, {}
-        llm, sums, neg_mean, std, z = {}, {}, {}, {}, {}
-        planes, n_grouped, n_codes, n_scales = {}, {}, {}, {}
+        x_words, x_grouped, x_codes, x_scales, x_acc = {}, {}, {}, {}, {}
+        llm, sums, neg_mean, std, z, z_ps = {}, {}, {}, {}, {}, {}
+        planes, n_grouped, n_codes, n_scales, n_acc = {}, {}, {}, {}, {}
 
-        def x_to_partitions(g):
+        def transpose_x(g):
+            x_words[g] = word_transposes(x_sb[g][:])
+
+        def copy_x(g):
             x_grouped[g] = work.tile([P, GROUP, PACK], BF16, name="x_grouped", align_bytes=64)
-            word_transposes(x_sb[g][:], x_grouped[g][:], False)
+            nc.scalar.copy(out=x_grouped[g][:].bitcast(F32), in_=x_words[g])
 
         def quantise_x(g):
             x_codes[g] = work.tile([P, GROUP], U32, name="x_codes", align_bytes=64)
             x_scales[g] = work.tile([P, GROUP], U8, name="x_scales", align_bytes=64)
             quantise(x_grouped[g][:], x_codes[g][:], x_scales[g][:])
 
-        def first_matmul(g):
-            llm[g] = wide.tile([P, TILES, D], F32, name="llm")
-            sums[g] = small.tile([P, TILES], F32, name="sums")
+        def multiply(codes, scales, w_codes, w_scales):
+            accs = []
             for j in range(TILES):
                 cols = slice(j * P, (j + 1) * P)
                 acc = psum_acc.tile([P, D], F32, name="acc", tag="acc")
                 nc.tensor.matmul_mx(
                     out=acc[:],
-                    lhsT=x_codes[g][:, cols].bitcast(FP8X4),
-                    lhsT_scale=x_scales[g][:, cols],
-                    rhs=w1_codes[:].bitcast(FP8X4),
-                    rhs_scale=w1_scales[:],
+                    lhsT=codes[:, cols].bitcast(FP8X4),
+                    lhsT_scale=scales[:, cols],
+                    rhs=w_codes[:].bitcast(FP8X4),
+                    rhs_scale=w_scales[:],
                     start=True,
                     stop=True,
                 )
+                accs.append(acc)
+            return accs
+
+        def first_matmul(g):
+            x_acc[g] = multiply(x_codes[g], x_scales[g], w1_codes, w1_scales)
+
+        def first_bias(g):
+            llm[g] = wide.tile([P, TILES, D], F32, name="llm")
+            sums[g] = small.tile([P, TILES], F32, name="sums")
+            for j in range(TILES):
                 nc.vector.scalar_tensor_tensor(
                     out=llm[g][:, j, :],
-                    in0=acc[:],
+                    in0=x_acc[g][j][:],
                     scalar=1.0,
                     in1=bias_bc[:, 0, :],
                     op0=ALU.mult,
@@ -223,31 +234,38 @@ def tile_crossfusion_pa_t_kernel(tc, x, w1, b1, gamma, beta, w2, b2, llm_out, q_
                     op1=ALU.mult,
                 )
 
-        def features_to_partitions(g):
-            planes[g] = work.tile([P, PACK, GROUP], BF16, name="planes")
+        def transpose_z(g):
+            z_ps[g] = []
             for h in range(2):
-                z_ps = psum_z.tile([P, 2, GROUP], F32, name="z_ps", tag="z_ps")
+                half = psum_z.tile([P, 2, GROUP], F32, name="z_ps", tag="z_ps")
                 for i in range(2):
                     t = 2 * h + i
                     for j in range(TILES):
                         nc.tensor.transpose(
-                            z_ps[:, i, j * P : (j + 1) * P], z[g][:, j, t * P : (t + 1) * P], ident_f32[:]
+                            half[:, i, j * P : (j + 1) * P], z[g][:, j, t * P : (t + 1) * P], ident_f32[:]
                         )
-                for i in range(2):
-                    t = 2 * h + i
-                    nc.scalar.activation(
-                        out=planes[g][:, t, :],
-                        in_=z_ps[:, i, :],
-                        func=ACT.Identity,
-                        bias=params[:, PACK + t : PACK + t + 1],
-                        scale=params[:, t : t + 1],
-                    )
+                z_ps[g].append(half)
+
+        def affine(g):
+            planes[g] = work.tile([P, PACK, GROUP], BF16, name="planes")
+            for t in range(PACK):
+                nc.scalar.activation(
+                    out=planes[g][:, t, :],
+                    in_=z_ps[g][t // 2][:, t % 2, :],
+                    func=ACT.Identity,
+                    bias=params[:, PACK + t : PACK + t + 1],
+                    scale=params[:, t : t + 1],
+                )
 
         def regroup_n(g):
             n_grouped[g] = work.tile([P, GROUP, PACK], BF16, name="n_grouped", align_bytes=64)
-            nc.vector.tensor_copy(
-                out=n_grouped[g][:].rearrange("p (c i) t -> p c t i", i=4),
-                in_=planes[g][:].rearrange("p t (c i) -> p c t i", i=4),
+            nc.gpsimd.tensor_scalar(
+                out=n_grouped[g][:],
+                in0=planes[g][:].rearrange("p t c -> p c t"),
+                scalar1=1.0,
+                scalar2=0.0,
+                op0=ALU.mult,
+                op1=ALU.add,
             )
 
         def quantise_n(g):
@@ -256,41 +274,39 @@ def tile_crossfusion_pa_t_kernel(tc, x, w1, b1, gamma, beta, w2, b2, llm_out, q_
             quantise(n_grouped[g][:], n_codes[g][:], n_scales[g][:])
 
         def second_matmul(g):
+            n_acc[g] = multiply(n_codes[g], n_scales[g], w2_codes, w2_scales)
+
+        def second_bias(g):
             q = wide.tile([P, TILES, D], F32)
             for j in range(TILES):
-                cols = slice(j * P, (j + 1) * P)
-                acc = psum_acc.tile([P, D], F32, name="acc", tag="acc")
-                nc.tensor.matmul_mx(
-                    out=acc[:],
-                    lhsT=n_codes[g][:, cols].bitcast(FP8X4),
-                    lhsT_scale=n_scales[g][:, cols],
-                    rhs=w2_codes[:].bitcast(FP8X4),
-                    rhs_scale=w2_scales[:],
-                    start=True,
-                    stop=True,
-                )
-                nc.vector.tensor_add(out=q[:, j, :], in0=acc[:], in1=bias_bc[:, 1, :])
+                nc.vector.tensor_add(out=q[:, j, :], in0=n_acc[g][j][:], in1=bias_bc[:, 1, :])
                 nc.sync.dma_start(out=q_groups[g][:, j, :], in_=q[:, j, :])
 
         def run(stage, g):
             if 0 <= g < GROUPS:
                 stage(g)
 
-        for step in range(GROUPS + LAST_LAG):
-            run(x_to_partitions, step)
-            run(regroup_n, step - 6)
-            run(quantise_x, step - 1)
-            run(quantise_n, step - 6)
-            run(normalise, step - 4)
-            run(first_matmul, step - 2)
-            run(second_matmul, step - 7)
-            run(statistics, step - 3)
-            run(features_to_partitions, step - 5)
-            if step == 0:
+        for step in range(-2, GROUPS + 3):
+            run(quantise_x, step)
+            run(quantise_n, step - 3)
+            run(first_matmul, step)
+            run(normalise, step - 1)
+            run(first_bias, step)
+            run(transpose_x, step + 2)
+            run(second_matmul, step - 3)
+            run(affine, step - 2)
+            run(regroup_n, step - 2)
+            run(copy_x, step + 1)
+            if step == 1:
+                w2_to_partitions()
+            run(transpose_z, step - 1)
+            run(second_bias, step - 3)
+            run(statistics, step)
+            if step == -1:
                 spread_bias(0)
                 turn_w2()
-            if step == W2_TRANSPOSE_STEP:
-                w2_to_partitions()
-            if step == W2_QUANTISE_STEP:
+            if step == 0:
+                params_to_partitions()
+            if step == 1:
                 quantise(w2_grouped[:], w2_codes[:], w2_scales[:])
                 spread_bias(1)

@@ -225,7 +225,7 @@ def tile_crossfusion_pa_t_kernel(tc, x, w1, b1, gamma, beta, w2, b2, llm_out, q_
             nc.vector.reciprocal(out=rstd[:], in_=std[g][:])
             z[g] = work.tile([P, TILES, D], F32, name="z")
             for j in range(TILES):
-                nc.gpsimd.tensor_scalar(
+                nc.vector.tensor_scalar(
                     out=unturned(z[g][:, j, :]),
                     in0=turn(llm[g][:, j, :]),
                     scalar1=neg_mean[g][:, j : j + 1],
@@ -290,10 +290,10 @@ def tile_crossfusion_pa_t_kernel(tc, x, w1, b1, gamma, beta, w2, b2, llm_out, q_
             run(quantise_x, step)
             run(quantise_n, step - 3)
             run(first_matmul, step)
+            run(second_matmul, step - 3)
             run(normalise, step - 1)
             run(first_bias, step)
             run(transpose_x, step + 2)
-            run(second_matmul, step - 3)
             run(affine, step - 2)
             run(regroup_n, step - 2)
             run(copy_x, step + 1)

@@ -35,8 +35,8 @@ def tile_crossfusion_pa_t_kernel(tc, x, w1, b1, gamma, beta, w2, b2, llm_out, q_
         const = stack.enter_context(tc.tile_pool(name="const", bufs=1))
         x_pool = stack.enter_context(tc.tile_pool(name="x_pool", bufs=GROUPS))
         work = stack.enter_context(tc.tile_pool(name="work", bufs=3))
-        wide = stack.enter_context(tc.tile_pool(name="wide", bufs=5))
-        small = stack.enter_context(tc.tile_pool(name="small", bufs=4))
+        wide = stack.enter_context(tc.tile_pool(name="wide", bufs=6))
+        small = stack.enter_context(tc.tile_pool(name="small", bufs=6))
         psum_t = stack.enter_context(tc.psum_pool(name="psum_t", bufs=2))
         psum_acc = stack.enter_context(tc.psum_pool(name="psum_acc", bufs=4))
         psum_z = stack.enter_context(tc.psum_pool(name="psum_z", bufs=2))
@@ -73,7 +73,7 @@ def tile_crossfusion_pa_t_kernel(tc, x, w1, b1, gamma, beta, w2, b2, llm_out, q_
         nc.vector.memset(ones[:], 1.0)
         warm = const.tile([P, 1], F32)
         nc.vector.memset(warm[:], 1.0)
-        nc.scalar.sqrt(out=warm[:], in_=warm[:])
+        nc.scalar.activation(out=warm[:], in_=warm[:], func=ACT.Abs_reciprocal_sqrt)
 
         def word_transposes(rows):
             words = rows.bitcast(F32)
@@ -153,7 +153,7 @@ def tile_crossfusion_pa_t_kernel(tc, x, w1, b1, gamma, beta, w2, b2, llm_out, q_
                 )
 
         x_words, x_grouped, x_codes, x_scales, x_acc = {}, {}, {}, {}, {}
-        llm, sums, neg_mean, std, z, z_ps = {}, {}, {}, {}, {}, {}
+        llm, sums, neg_mean, sum_sq, rstd, z, z_ps = {}, {}, {}, {}, {}, {}, {}
         planes, n_grouped, n_codes, n_scales, n_acc = {}, {}, {}, {}, {}
 
         def transpose_x(g):
@@ -203,33 +203,37 @@ def tile_crossfusion_pa_t_kernel(tc, x, w1, b1, gamma, beta, w2, b2, llm_out, q_
                 )
             nc.sync.dma_start(out=llm_groups[g], in_=llm[g][:])
 
-        def statistics(g):
+        def mean(g):
             neg_mean[g] = small.tile([P, TILES], F32, name="neg_mean")
             nc.scalar.mul(out=neg_mean[g][:], in_=sums[g][:], mul=-1.0 / D)
-            squares = work.tile([P, TILES, D], BF16)
-            sum_sq = small.tile([P, TILES], F32)
+
+        def squares(g):
+            deviations = work.tile([P, TILES, D], BF16, name="deviations")
+            sum_sq[g] = small.tile([P, TILES], F32, name="sum_sq")
             for j in range(TILES):
                 nc.scalar.activation(
-                    out=squares[:, j, :],
+                    out=deviations[:, j, :],
                     in_=llm[g][:, j, :],
                     func=ACT.Square,
                     bias=neg_mean[g][:, j : j + 1],
                     scale=1.0,
-                    accum_out=sum_sq[:, j : j + 1],
+                    accum_out=sum_sq[g][:, j : j + 1],
                 )
-            std[g] = small.tile([P, TILES], F32, name="std")
-            nc.scalar.activation(out=std[g][:], in_=sum_sq[:], func=ACT.Sqrt, bias=EPS, scale=1.0 / D)
+
+        def inverse_deviation(g):
+            rstd[g] = small.tile([P, TILES], F32, name="rstd")
+            nc.scalar.activation(
+                out=rstd[g][:], in_=sum_sq[g][:], func=ACT.Abs_reciprocal_sqrt, bias=EPS, scale=1.0 / D
+            )
 
         def normalise(g):
-            rstd = small.tile([P, TILES], F32)
-            nc.vector.reciprocal(out=rstd[:], in_=std[g][:])
             z[g] = work.tile([P, TILES, D], F32, name="z")
             for j in range(TILES):
                 nc.vector.tensor_scalar(
                     out=unturned(z[g][:, j, :]),
                     in0=turn(llm[g][:, j, :]),
                     scalar1=neg_mean[g][:, j : j + 1],
-                    scalar2=rstd[:, j : j + 1],
+                    scalar2=rstd[g][:, j : j + 1],
                     op0=ALU.add,
                     op1=ALU.mult,
                 )
@@ -286,27 +290,29 @@ def tile_crossfusion_pa_t_kernel(tc, x, w1, b1, gamma, beta, w2, b2, llm_out, q_
             if 0 <= g < GROUPS:
                 stage(g)
 
-        for step in range(-2, GROUPS + 3):
-            run(quantise_x, step)
-            run(quantise_n, step - 3)
+        for step in range(-3, GROUPS + 6):
+            run(normalise, step - 3)
+            run(regroup_n, step - 5)
+            run(mean, step - 1)
             run(first_matmul, step)
-            run(second_matmul, step - 3)
-            run(normalise, step - 1)
+            run(affine, step - 4)
+            run(second_matmul, step - 6)
+            run(transpose_x, step + 3)
+            run(copy_x, step + 2)
+            run(quantise_n, step - 5)
+            run(inverse_deviation, step - 2)
+            run(quantise_x, step + 1)
+            run(transpose_z, step - 3)
             run(first_bias, step)
-            run(transpose_x, step + 2)
-            run(affine, step - 2)
-            run(regroup_n, step - 2)
-            run(copy_x, step + 1)
-            if step == 1:
-                w2_to_partitions()
-            run(transpose_z, step - 1)
-            run(second_bias, step - 3)
-            run(statistics, step)
-            if step == -1:
+            run(squares, step - 1)
+            run(second_bias, step - 6)
+            if step == -2:
                 spread_bias(0)
                 turn_w2()
             if step == 0:
                 params_to_partitions()
-            if step == 1:
-                quantise(w2_grouped[:], w2_codes[:], w2_scales[:])
+            if step == 2:
+                w2_to_partitions()
                 spread_bias(1)
+            if step == 3:
+                quantise(w2_grouped[:], w2_codes[:], w2_scales[:])

@@ -18,7 +18,9 @@ TOKENS = 16 * 256
 TILES = 2
 GROUP = P * TILES
 GROUPS = TOKENS // GROUP
+HALF = D // 2
 RUN = 8
+FIRST_ON_SCALAR = 4
 EPS = 1e-5
 
 FLOPS = 2 * 2 * TOKENS * D * D
@@ -48,21 +50,22 @@ def tile_crossfusion_pa_t_kernel(tc, x, w1, b1, gamma, beta, w2, b2, llm_out, q_
         w2_sb = const.tile([P, PACK, D], BF16)
         bias_rows = const.tile([P, 2, D], BF16)
         param_rows = const.tile([P, P], BF16)
-        nc.vector.memset(bias_rows[:], 0.0)
-        nc.vector.memset(param_rows[:], 0.0)
-        nc.sync.dma_start(out=w1_sb[:], in_=w1.rearrange("(ob p) k -> p ob k", p=P))
-        nc.sync.dma_start(out=x_sb[0][:], in_=x_groups[0])
-        nc.sync.dma_start(out=bias_rows[0:1, 0, :], in_=b1.rearrange("(o f) -> o f", o=1))
-        nc.sync.dma_start(out=x_sb[1][:], in_=x_groups[1])
-        nc.sync.dma_start(out=x_sb[2][:], in_=x_groups[2])
-        nc.sync.dma_start(out=w2_sb[:], in_=w2.rearrange("(ob p) k -> p ob k", p=P))
-        nc.sync.dma_start(out=bias_rows[0:1, 1, :], in_=b2.rearrange("(o f) -> o f", o=1))
+        nc.vector.memset(bias_rows[:, 0, :].bitcast(F32), 0.0)
+        nc.vector.memset(bias_rows[:, 1, :].bitcast(F32), 0.0)
+        nc.vector.memset(param_rows[:].bitcast(F32), 0.0)
+        w1_blocks = w1.rearrange("(ob p) k -> p ob k", p=P)
+        nc.sync.dma_start(out=w1_sb[:, 0:2, :], in_=w1_blocks[:, 0:2, :])
+        nc.sync.dma_start(out=w1_sb[:, 2:4, :], in_=w1_blocks[:, 2:4, :])
+        for i, bias in enumerate((b1, b2)):
+            nc.scalar.dma_start(out=bias_rows[0:1, i, :], in_=bias.rearrange("(o f) -> o f", o=1))
         for n, vec in enumerate((gamma, beta)):
-            nc.sync.dma_start(
+            nc.scalar.dma_start(
                 out=param_rows[n * PACK : (n + 1) * PACK, :].rearrange("t (s i) -> t s i", i=RUN),
                 in_=vec.rearrange("(s t i) -> t s i", t=PACK, i=RUN),
             )
-        for g in range(3, GROUPS):
+        for g in range(GROUPS):
+            if g == 4:
+                nc.sync.dma_start(out=w2_sb[:], in_=w2.rearrange("(ob p) k -> p ob k", p=P))
             nc.sync.dma_start(out=x_sb[g][:], in_=x_groups[g])
 
         ident_f32 = const.tile([P, P], F32)
@@ -101,13 +104,17 @@ def tile_crossfusion_pa_t_kernel(tc, x, w1, b1, gamma, beta, w2, b2, llm_out, q_
         w1_grouped = const.tile([P, D, PACK], BF16, align_bytes=64)
         w1_codes = const.tile([P, D], U32, align_bytes=64)
         w1_scales = const.tile([P, D], U8, align_bytes=64)
-        nc.vector.tensor_copy(
-            out=w1_grouped[:, 0 : 2 * P, :].bitcast(F32), in_=word_transposes(w1_sb[:, 0:2, :])
-        )
-        nc.scalar.copy(
-            out=w1_grouped[:, 2 * P : 4 * P, :].bitcast(F32), in_=word_transposes(w1_sb[:, 2:4, :])
-        )
-        quantise(w1_grouped[:], w1_codes[:], w1_scales[:])
+        def w1_half(h):
+            cols = slice(h * HALF, (h + 1) * HALF)
+            words = word_transposes(w1_sb[:, 2 * h : 2 * h + 2, :])
+            if h == 0:
+                nc.vector.tensor_copy(out=w1_grouped[:, cols, :].bitcast(F32), in_=words)
+            else:
+                nc.scalar.copy(out=w1_grouped[:, cols, :].bitcast(F32), in_=words)
+
+        def quantise_w1_half(h):
+            cols = slice(h * HALF, (h + 1) * HALF)
+            quantise(w1_grouped[:, cols, :], w1_codes[:, cols], w1_scales[:, cols])
 
         bias_bc = const.tile([P, 2, D], F32)
         params = const.tile([P, 2 * PACK], F32)
@@ -130,30 +137,29 @@ def tile_crossfusion_pa_t_kernel(tc, x, w1, b1, gamma, beta, w2, b2, llm_out, q_
         def spread_bias(i):
             bias_ps = psum_acc.tile([P, D], F32, name="bias_ps", tag="acc")
             nc.tensor.matmul(bias_ps[:], lhsT=ones[:], rhs=bias_rows[:, i, :], start=True, stop=True)
-            nc.vector.tensor_copy(out=bias_bc[:, i, :], in_=bias_ps[:])
+            nc.scalar.copy(out=bias_bc[:, i, :], in_=bias_ps[:])
 
         def params_to_partitions():
             param_ps = psum_t.tile([P, P], BF16, name="param_ps", tag="tp")
             nc.tensor.transpose(param_ps[:], param_rows[:], ident_bf[:])
             nc.scalar.copy(out=params[:], in_=param_ps[:, 0 : 2 * PACK])
 
-        def w2_to_partitions():
-            for h in range(2):
-                w2_ps = psum_z.tile([P, PACK, 2 * P], BF16, name="w2_ps", tag="z_ps")
-                for b in range(2):
-                    for t in range(PACK):
-                        nc.tensor.transpose(
-                            w2_ps[:, t, b * P : (b + 1) * P],
-                            w2_turned[:, 2 * h + b, t * P : (t + 1) * P],
-                            ident_bf[:],
-                        )
-                nc.scalar.copy(
-                    out=w2_grouped[:, 2 * h * P : 2 * (h + 1) * P, :],
-                    in_=w2_ps[:].rearrange("p t c -> p c t"),
-                )
+        def w2_half(h):
+            w2_ps = psum_acc.tile([P, PACK, HALF], BF16, name="w2_ps", tag="acc")
+            for b in range(2):
+                for t in range(PACK):
+                    nc.tensor.transpose(
+                        w2_ps[:, t, b * P : (b + 1) * P],
+                        w2_turned[:, 2 * h + b, t * P : (t + 1) * P],
+                        ident_bf[:],
+                    )
+            nc.scalar.copy(
+                out=w2_grouped[:, h * HALF : (h + 1) * HALF, :],
+                in_=w2_ps[:].rearrange("p t c -> p c t"),
+            )
 
         x_words, x_grouped, x_codes, x_scales, x_acc = {}, {}, {}, {}, {}
-        llm, sums, neg_mean, sum_sq, rstd, z, z_ps = {}, {}, {}, {}, {}, {}, {}
+        llm, sums, neg_mean, sum_sq, rstd, shift, z, z_ps = {}, {}, {}, {}, {}, {}, {}, {}
         planes, n_grouped, n_codes, n_scales, n_acc = {}, {}, {}, {}, {}
 
         def transpose_x(g):
@@ -161,7 +167,10 @@ def tile_crossfusion_pa_t_kernel(tc, x, w1, b1, gamma, beta, w2, b2, llm_out, q_
 
         def copy_x(g):
             x_grouped[g] = work.tile([P, GROUP, PACK], BF16, name="x_grouped", align_bytes=64)
-            nc.scalar.copy(out=x_grouped[g][:].bitcast(F32), in_=x_words[g])
+            if g == 0:
+                nc.vector.tensor_copy(out=x_grouped[g][:].bitcast(F32), in_=x_words[g])
+            else:
+                nc.scalar.copy(out=x_grouped[g][:].bitcast(F32), in_=x_words[g])
 
         def quantise_x(g):
             x_codes[g] = work.tile([P, GROUP], U32, name="x_codes", align_bytes=64)
@@ -226,17 +235,36 @@ def tile_crossfusion_pa_t_kernel(tc, x, w1, b1, gamma, beta, w2, b2, llm_out, q_
                 out=rstd[g][:], in_=sum_sq[g][:], func=ACT.Abs_reciprocal_sqrt, bias=EPS, scale=1.0 / D
             )
 
+        def on_scalar(g, j):
+            return j == 1 and g % 2 == 0 and g >= FIRST_ON_SCALAR
+
+        def shift_of(g):
+            if on_scalar(g, 1):
+                shift[g] = small.tile([P, 1], F32, name="shift")
+                nc.scalar.activation(
+                    out=shift[g][:], in_=neg_mean[g][:, 1:2], func=ACT.Identity, scale=rstd[g][:, 1:2]
+                )
+
         def normalise(g):
             z[g] = work.tile([P, TILES, D], F32, name="z")
             for j in range(TILES):
-                nc.vector.tensor_scalar(
-                    out=unturned(z[g][:, j, :]),
-                    in0=turn(llm[g][:, j, :]),
-                    scalar1=neg_mean[g][:, j : j + 1],
-                    scalar2=rstd[g][:, j : j + 1],
-                    op0=ALU.add,
-                    op1=ALU.mult,
-                )
+                if on_scalar(g, j):
+                    nc.scalar.activation(
+                        out=unturned(z[g][:, j, :]),
+                        in_=turn(llm[g][:, j, :]),
+                        func=ACT.Identity,
+                        bias=shift[g][:],
+                        scale=rstd[g][:, j : j + 1],
+                    )
+                else:
+                    nc.vector.tensor_scalar(
+                        out=unturned(z[g][:, j, :]),
+                        in0=turn(llm[g][:, j, :]),
+                        scalar1=neg_mean[g][:, j : j + 1],
+                        scalar2=rstd[g][:, j : j + 1],
+                        op0=ALU.add,
+                        op1=ALU.mult,
+                    )
 
         def transpose_z(g):
             z_ps[g] = []
@@ -290,7 +318,15 @@ def tile_crossfusion_pa_t_kernel(tc, x, w1, b1, gamma, beta, w2, b2, llm_out, q_
             if 0 <= g < GROUPS:
                 stage(g)
 
-        for step in range(-3, GROUPS + 6):
+        w1_half(0)
+        w1_half(1)
+        transpose_x(0)
+        spread_bias(0)
+        quantise_w1_half(0)
+        quantise_w1_half(1)
+        copy_x(0)
+
+        for step in range(-2, GROUPS + 6):
             run(normalise, step - 3)
             run(regroup_n, step - 5)
             run(mean, step - 1)
@@ -298,21 +334,22 @@ def tile_crossfusion_pa_t_kernel(tc, x, w1, b1, gamma, beta, w2, b2, llm_out, q_
             run(affine, step - 4)
             run(second_matmul, step - 6)
             run(transpose_x, step + 3)
-            run(copy_x, step + 2)
+            if step > -2:
+                run(copy_x, step + 2)
             run(quantise_n, step - 5)
             run(inverse_deviation, step - 2)
             run(quantise_x, step + 1)
             run(transpose_z, step - 3)
             run(first_bias, step)
             run(squares, step - 1)
+            run(shift_of, step - 2)
             run(second_bias, step - 6)
             if step == -2:
-                spread_bias(0)
                 turn_w2()
             if step == 0:
                 params_to_partitions()
-            if step == 2:
-                w2_to_partitions()
+            if step in (2, 3):
+                w2_half(step - 2)
+            if step == 4:
                 spread_bias(1)
-            if step == 3:
                 quantise(w2_grouped[:], w2_codes[:], w2_scales[:])

@@ -21,6 +21,7 @@ GROUPS = TOKENS // GROUP
 HALF = D // 2
 RUN = 8
 FIRST_ON_SCALAR = 4
+WARM_UP = 4
 EPS = 1e-5
 
 FLOPS = 2 * 2 * TOKENS * D * D
@@ -100,6 +101,12 @@ def tile_crossfusion_pa_t_kernel(tc, x, w1, b1, gamma, beta, w2, b2, llm_out, q_
 
         def unturned(features):
             return features.rearrange("p (t s i) -> p t s i", t=PACK, i=RUN)
+
+        idle_rows = const.tile([P, D], BF16)
+        nc.vector.memset(idle_rows[:].bitcast(F32), 0.0)
+        idle_ps = psum_acc.tile([P, D], F32, name="idle_ps", tag="acc")
+        for n in range(WARM_UP):
+            nc.tensor.matmul(idle_ps[:], lhsT=idle_rows[:, 0:P], rhs=idle_rows[:], start=True, stop=True)
 
         w1_grouped = const.tile([P, D, PACK], BF16, align_bytes=64)
         w1_codes = const.tile([P, D], U32, align_bytes=64)

@@ -18,10 +18,11 @@ TOKENS = 16 * 256
 TILES = 2
 GROUP = P * TILES
 GROUPS = TOKENS // GROUP
+LAG = 6
 HALF = D // 2
 RUN = 8
 FIRST_ON_SCALAR = 4
-WARM_UP = 4
+WARM_UP = 3
 EPS = 1e-5
 
 FLOPS = 2 * 2 * TOKENS * D * D
@@ -37,7 +38,7 @@ def tile_crossfusion_pa_t_kernel(tc, x, w1, b1, gamma, beta, w2, b2, llm_out, q_
         stack.enter_context(tc.manual_schedule())
         const = stack.enter_context(tc.tile_pool(name="const", bufs=1))
         x_pool = stack.enter_context(tc.tile_pool(name="x_pool", bufs=GROUPS))
-        work = stack.enter_context(tc.tile_pool(name="work", bufs=3))
+        work = stack.enter_context(tc.tile_pool(name="work", bufs=4))
         wide = stack.enter_context(tc.tile_pool(name="wide", bufs=6))
         small = stack.enter_context(tc.tile_pool(name="small", bufs=6))
         psum_t = stack.enter_context(tc.psum_pool(name="psum_t", bufs=2))
@@ -51,6 +52,11 @@ def tile_crossfusion_pa_t_kernel(tc, x, w1, b1, gamma, beta, w2, b2, llm_out, q_
         w2_sb = const.tile([P, PACK, D], BF16)
         bias_rows = const.tile([P, 2, D], BF16)
         param_rows = const.tile([P, P], BF16)
+        warm = const.tile([P, 1], F32)
+        nc.vector.memset(warm[:], 1.0)
+        nc.scalar.activation(out=warm[:], in_=warm[:], func=ACT.Abs_reciprocal_sqrt)
+        idle_rows = const.tile([P, D], BF16)
+        nc.vector.memset(idle_rows[:].bitcast(F32), 0.0)
         nc.vector.memset(bias_rows[:, 0, :].bitcast(F32), 0.0)
         nc.vector.memset(bias_rows[:, 1, :].bitcast(F32), 0.0)
         nc.vector.memset(param_rows[:].bitcast(F32), 0.0)
@@ -75,9 +81,6 @@ def tile_crossfusion_pa_t_kernel(tc, x, w1, b1, gamma, beta, w2, b2, llm_out, q_
         make_identity(nc, ident_bf[:])
         ones = const.tile([P, P], BF16)
         nc.vector.memset(ones[:], 1.0)
-        warm = const.tile([P, 1], F32)
-        nc.vector.memset(warm[:], 1.0)
-        nc.scalar.activation(out=warm[:], in_=warm[:], func=ACT.Abs_reciprocal_sqrt)
 
         def word_transposes(rows):
             words = rows.bitcast(F32)
@@ -102,8 +105,6 @@ def tile_crossfusion_pa_t_kernel(tc, x, w1, b1, gamma, beta, w2, b2, llm_out, q_
         def unturned(features):
             return features.rearrange("p (t s i) -> p t s i", t=PACK, i=RUN)
 
-        idle_rows = const.tile([P, D], BF16)
-        nc.vector.memset(idle_rows[:].bitcast(F32), 0.0)
         idle_ps = psum_acc.tile([P, D], F32, name="idle_ps", tag="acc")
         for n in range(WARM_UP):
             nc.tensor.matmul(idle_ps[:], lhsT=idle_rows[:, 0:P], rhs=idle_rows[:], start=True, stop=True)
@@ -165,29 +166,39 @@ def tile_crossfusion_pa_t_kernel(tc, x, w1, b1, gamma, beta, w2, b2, llm_out, q_
                 in_=w2_ps[:].rearrange("p t c -> p c t"),
             )
 
-        x_words, x_grouped, x_codes, x_scales, x_acc = {}, {}, {}, {}, {}
+        pairs, pair_codes, pair_scales = {}, {}, {}
+        halves = (slice(0, GROUP), slice(GROUP, 2 * GROUP))
+        x_words, x_acc = {}, {}
         llm, sums, neg_mean, sum_sq, rstd, shift, z, z_ps = {}, {}, {}, {}, {}, {}, {}, {}
-        planes, n_grouped, n_codes, n_scales, n_acc = {}, {}, {}, {}, {}
+        planes, n_acc = {}, {}
+
+        def pair(a):
+            if a not in pairs:
+                pairs[a] = work.tile([P, 2 * GROUP, PACK], BF16, name="pair", align_bytes=64)
+            return pairs[a]
 
         def transpose_x(g):
             x_words[g] = word_transposes(x_sb[g][:])
 
         def copy_x(g):
-            x_grouped[g] = work.tile([P, GROUP, PACK], BF16, name="x_grouped", align_bytes=64)
+            out = pair(g)[:, halves[0], :].rearrange("p c t -> p (c t)").bitcast(F32)
+            out = out.rearrange("p (c u) -> p c u", u=2)
             if g == 0:
-                nc.vector.tensor_copy(out=x_grouped[g][:].bitcast(F32), in_=x_words[g])
+                nc.vector.tensor_copy(out=out, in_=x_words[g])
             else:
-                nc.scalar.copy(out=x_grouped[g][:].bitcast(F32), in_=x_words[g])
+                nc.scalar.copy(out=out, in_=x_words[g])
 
-        def quantise_x(g):
-            x_codes[g] = work.tile([P, GROUP], U32, name="x_codes", align_bytes=64)
-            x_scales[g] = work.tile([P, GROUP], U8, name="x_scales", align_bytes=64)
-            quantise(x_grouped[g][:], x_codes[g][:], x_scales[g][:])
+        def quantise_pair(a):
+            cols = slice(0 if a < GROUPS else GROUP, 2 * GROUP if a >= LAG else GROUP)
+            pair_codes[a] = work.tile([P, 2 * GROUP], U32, name="pair_codes", align_bytes=64)
+            pair_scales[a] = work.tile([P, 2 * GROUP], U8, name="pair_scales", align_bytes=64)
+            quantise(pairs[a][:, cols, :], pair_codes[a][:, cols], pair_scales[a][:, cols])
 
-        def multiply(codes, scales, w_codes, w_scales):
+        def multiply(a, half, w_codes, w_scales):
+            codes, scales = pair_codes[a], pair_scales[a]
             accs = []
             for j in range(TILES):
-                cols = slice(j * P, (j + 1) * P)
+                cols = slice(half * GROUP + j * P, half * GROUP + (j + 1) * P)
                 acc = psum_acc.tile([P, D], F32, name="acc", tag="acc")
                 nc.tensor.matmul_mx(
                     out=acc[:],
@@ -202,7 +213,7 @@ def tile_crossfusion_pa_t_kernel(tc, x, w1, b1, gamma, beta, w2, b2, llm_out, q_
             return accs
 
         def first_matmul(g):
-            x_acc[g] = multiply(x_codes[g], x_scales[g], w1_codes, w1_scales)
+            x_acc[g] = multiply(g, 0, w1_codes, w1_scales)
 
         def first_bias(g):
             llm[g] = wide.tile([P, TILES, D], F32, name="llm")
@@ -297,9 +308,8 @@ def tile_crossfusion_pa_t_kernel(tc, x, w1, b1, gamma, beta, w2, b2, llm_out, q_
                 )
 
         def regroup_n(g):
-            n_grouped[g] = work.tile([P, GROUP, PACK], BF16, name="n_grouped", align_bytes=64)
             nc.gpsimd.tensor_scalar(
-                out=n_grouped[g][:],
+                out=pair(g + LAG)[:, halves[1], :],
                 in0=planes[g][:].rearrange("p t c -> p c t"),
                 scalar1=1.0,
                 scalar2=0.0,
@@ -307,13 +317,8 @@ def tile_crossfusion_pa_t_kernel(tc, x, w1, b1, gamma, beta, w2, b2, llm_out, q_
                 op1=ALU.add,
             )
 
-        def quantise_n(g):
-            n_codes[g] = work.tile([P, GROUP], U32, name="n_codes", align_bytes=64)
-            n_scales[g] = work.tile([P, GROUP], U8, name="n_scales", align_bytes=64)
-            quantise(n_grouped[g][:], n_codes[g][:], n_scales[g][:])
-
         def second_matmul(g):
-            n_acc[g] = multiply(n_codes[g], n_scales[g], w2_codes, w2_scales)
+            n_acc[g] = multiply(g + LAG, 1, w2_codes, w2_scales)
 
         def second_bias(g):
             q = wide.tile([P, TILES, D], F32)
@@ -330,8 +335,8 @@ def tile_crossfusion_pa_t_kernel(tc, x, w1, b1, gamma, beta, w2, b2, llm_out, q_
         transpose_x(0)
         spread_bias(0)
         quantise_w1_half(0)
-        quantise_w1_half(1)
         copy_x(0)
+        quantise_w1_half(1)
 
         for step in range(-2, GROUPS + 6):
             run(normalise, step - 3)
@@ -343,9 +348,9 @@ def tile_crossfusion_pa_t_kernel(tc, x, w1, b1, gamma, beta, w2, b2, llm_out, q_
             run(transpose_x, step + 3)
             if step > -2:
                 run(copy_x, step + 2)
-            run(quantise_n, step - 5)
             run(inverse_deviation, step - 2)
-            run(quantise_x, step + 1)
+            if 0 <= step + 1 < GROUPS + LAG:
+                quantise_pair(step + 1)
             run(transpose_z, step - 3)
             run(first_bias, step)
             run(squares, step - 1)

@@ -344,8 +344,8 @@ def tile_crossfusion_pa_t_kernel(tc, x, w1, b1, gamma, beta, w2, b2, llm_out, q_
             run(mean, step - 1)
             run(first_matmul, step)
             run(affine, step - 4)
-            run(second_matmul, step - 6)
             run(transpose_x, step + 3)
+            run(second_matmul, step - 6)
             if step > -2:
                 run(copy_x, step + 2)
             run(inverse_deviation, step - 2)

@@ -21,7 +21,6 @@ GROUPS = TOKENS // GROUP
 LAG = 6
 HALF = D // 2
 RUN = 8
-FIRST_ON_SCALAR = 4
 WARM_UP = 3
 EPS = 1e-5
 
@@ -39,11 +38,12 @@ def tile_crossfusion_pa_t_kernel(tc, x, w1, b1, gamma, beta, w2, b2, llm_out, q_
         const = stack.enter_context(tc.tile_pool(name="const", bufs=1))
         x_pool = stack.enter_context(tc.tile_pool(name="x_pool", bufs=GROUPS))
         work = stack.enter_context(tc.tile_pool(name="work", bufs=4))
-        wide = stack.enter_context(tc.tile_pool(name="wide", bufs=6))
-        small = stack.enter_context(tc.tile_pool(name="small", bufs=6))
+        wide = stack.enter_context(tc.tile_pool(name="wide", bufs=7))
+        n_pool = stack.enter_context(tc.tile_pool(name="n_pool", bufs=2))
+        small = stack.enter_context(tc.tile_pool(name="small", bufs=7))
         psum_t = stack.enter_context(tc.psum_pool(name="psum_t", bufs=2))
-        psum_acc = stack.enter_context(tc.psum_pool(name="psum_acc", bufs=4))
-        psum_z = stack.enter_context(tc.psum_pool(name="psum_z", bufs=2))
+        psum_acc = stack.enter_context(tc.psum_pool(name="psum_acc", bufs=3))
+        psum_z = stack.enter_context(tc.psum_pool(name="psum_z", bufs=3))
 
         x_sb = []
         for g in range(GROUPS):
@@ -166,39 +166,39 @@ def tile_crossfusion_pa_t_kernel(tc, x, w1, b1, gamma, beta, w2, b2, llm_out, q_
                 in_=w2_ps[:].rearrange("p t c -> p c t"),
             )
 
-        pairs, pair_codes, pair_scales = {}, {}, {}
-        halves = (slice(0, GROUP), slice(GROUP, 2 * GROUP))
+        grouped, codes_of, scales_of = {}, {}, {}
         x_words, x_acc = {}, {}
         llm, sums, neg_mean, sum_sq, rstd, shift, z, z_ps = {}, {}, {}, {}, {}, {}, {}, {}
         planes, n_acc = {}, {}
-
-        def pair(a):
-            if a not in pairs:
-                pairs[a] = work.tile([P, 2 * GROUP, PACK], BF16, name="pair", align_bytes=64)
-            return pairs[a]
 
         def transpose_x(g):
             x_words[g] = word_transposes(x_sb[g][:])
 
         def copy_x(g):
-            out = pair(g)[:, halves[0], :].rearrange("p c t -> p (c t)").bitcast(F32)
+            grouped["x", g] = work.tile([P, GROUP, PACK], BF16, name="x_grouped", align_bytes=64)
+            out = grouped["x", g][:].rearrange("p c t -> p (c t)").bitcast(F32)
             out = out.rearrange("p (c u) -> p c u", u=2)
             if g == 0:
                 nc.vector.tensor_copy(out=out, in_=x_words[g])
             else:
                 nc.scalar.copy(out=out, in_=x_words[g])
 
-        def quantise_pair(a):
-            cols = slice(0 if a < GROUPS else GROUP, 2 * GROUP if a >= LAG else GROUP)
-            pair_codes[a] = work.tile([P, 2 * GROUP], U32, name="pair_codes", align_bytes=64)
-            pair_scales[a] = work.tile([P, 2 * GROUP], U8, name="pair_scales", align_bytes=64)
-            quantise(pairs[a][:, cols, :], pair_codes[a][:, cols], pair_scales[a][:, cols])
+        def quantise_group(kind, g):
+            codes_of[kind, g] = work.tile([P, GROUP], U32, name="codes", tag=kind + "_codes", align_bytes=64)
+            scales_of[kind, g] = work.tile([P, GROUP], U8, name="scales", tag=kind + "_scales", align_bytes=64)
+            quantise(grouped[kind, g][:], codes_of[kind, g][:], scales_of[kind, g][:])
 
-        def multiply(a, half, w_codes, w_scales):
-            codes, scales = pair_codes[a], pair_scales[a]
+        def quantise_x(g):
+            quantise_group("x", g)
+
+        def quantise_n(g):
+            quantise_group("n", g)
+
+        def multiply(kind, g, w_codes, w_scales):
+            codes, scales = codes_of[kind, g], scales_of[kind, g]
             accs = []
             for j in range(TILES):
-                cols = slice(half * GROUP + j * P, half * GROUP + (j + 1) * P)
+                cols = slice(j * P, (j + 1) * P)
                 acc = psum_acc.tile([P, D], F32, name="acc", tag="acc")
                 nc.tensor.matmul_mx(
                     out=acc[:],
@@ -213,7 +213,7 @@ def tile_crossfusion_pa_t_kernel(tc, x, w1, b1, gamma, beta, w2, b2, llm_out, q_
             return accs
 
         def first_matmul(g):
-            x_acc[g] = multiply(g, 0, w1_codes, w1_scales)
+            x_acc[g] = multiply("x", g, w1_codes, w1_scales)
 
         def first_bias(g):
             llm[g] = wide.tile([P, TILES, D], F32, name="llm")
@@ -242,19 +242,19 @@ def tile_crossfusion_pa_t_kernel(tc, x, w1, b1, gamma, beta, w2, b2, llm_out, q_
                     out=deviations[:, j, :],
                     in_=llm[g][:, j, :],
                     func=ACT.Square,
-                    bias=neg_mean[g][:, j : j + 1],
-                    scale=1.0,
+                    bias=sums[g][:, j : j + 1],
+                    scale=-float(D),
                     accum_out=sum_sq[g][:, j : j + 1],
                 )
 
         def inverse_deviation(g):
             rstd[g] = small.tile([P, TILES], F32, name="rstd")
             nc.scalar.activation(
-                out=rstd[g][:], in_=sum_sq[g][:], func=ACT.Abs_reciprocal_sqrt, bias=EPS, scale=1.0 / D
+                out=rstd[g][:], in_=sum_sq[g][:], func=ACT.Abs_reciprocal_sqrt, bias=EPS, scale=1.0 / D**3
             )
 
         def on_scalar(g, j):
-            return j == 1 and g % 2 == 0 and g >= FIRST_ON_SCALAR
+            return j == 1 and g % 4 != 3 and 4 <= g < 14
 
         def shift_of(g):
             if on_scalar(g, 1):
@@ -308,17 +308,24 @@ def tile_crossfusion_pa_t_kernel(tc, x, w1, b1, gamma, beta, w2, b2, llm_out, q_
                 )
 
         def regroup_n(g):
+            grouped["n", g] = n_pool.tile([P, GROUP, PACK], BF16, name="n_grouped", align_bytes=64)
+            columns = P if g >= 13 else GROUP
             nc.gpsimd.tensor_scalar(
-                out=pair(g + LAG)[:, halves[1], :],
-                in0=planes[g][:].rearrange("p t c -> p c t"),
+                out=grouped["n", g][:, 0:columns, :],
+                in0=planes[g][:, :, 0:columns].rearrange("p t c -> p c t"),
                 scalar1=1.0,
                 scalar2=0.0,
                 op0=ALU.mult,
                 op1=ALU.add,
             )
+            if columns < GROUP:
+                nc.scalar.copy(
+                    out=grouped["n", g][:, columns:GROUP, :],
+                    in_=planes[g][:, :, columns:GROUP].rearrange("p t c -> p c t"),
+                )
 
         def second_matmul(g):
-            n_acc[g] = multiply(g + LAG, 1, w2_codes, w2_scales)
+            n_acc[g] = multiply("n", g, w2_codes, w2_scales)
 
         def second_bias(g):
             q = wide.tile([P, TILES, D], F32)
@@ -338,30 +345,31 @@ def tile_crossfusion_pa_t_kernel(tc, x, w1, b1, gamma, beta, w2, b2, llm_out, q_
         copy_x(0)
         quantise_w1_half(1)
 
-        for step in range(-2, GROUPS + 6):
-            run(normalise, step - 3)
+        for step in range(-2, GROUPS + LAG):
             run(regroup_n, step - 5)
-            run(mean, step - 1)
             run(first_matmul, step)
             run(affine, step - 4)
             run(transpose_x, step + 3)
-            run(second_matmul, step - 6)
             if step > -2:
                 run(copy_x, step + 2)
             run(inverse_deviation, step - 2)
-            if 0 <= step + 1 < GROUPS + LAG:
-                quantise_pair(step + 1)
+            run(normalise, step - 3)
+            run(second_matmul, step - 6)
+            run(quantise_n, step - 5)
+            run(quantise_x, step + 1)
             run(transpose_z, step - 3)
             run(first_bias, step)
+            run(mean, step - 2)
             run(squares, step - 1)
             run(shift_of, step - 2)
             run(second_bias, step - 6)
             if step == -2:
                 turn_w2()
-            if step == 0:
+            if step == 1:
                 params_to_partitions()
             if step in (2, 3):
                 w2_half(step - 2)
             if step == 4:
-                spread_bias(1)
                 quantise(w2_grouped[:], w2_codes[:], w2_scales[:])
+            if step == 5:
+                spread_bias(1)

@@ -39,7 +39,6 @@ def tile_crossfusion_pa_t_kernel(tc, x, w1, b1, gamma, beta, w2, b2, llm_out, q_
         x_pool = stack.enter_context(tc.tile_pool(name="x_pool", bufs=GROUPS))
         work = stack.enter_context(tc.tile_pool(name="work", bufs=4))
         wide = stack.enter_context(tc.tile_pool(name="wide", bufs=7))
-        n_pool = stack.enter_context(tc.tile_pool(name="n_pool", bufs=2))
         small = stack.enter_context(tc.tile_pool(name="small", bufs=7))
         psum_t = stack.enter_context(tc.psum_pool(name="psum_t", bufs=2))
         psum_acc = stack.enter_context(tc.psum_pool(name="psum_acc", bufs=3))
@@ -61,6 +60,7 @@ def tile_crossfusion_pa_t_kernel(tc, x, w1, b1, gamma, beta, w2, b2, llm_out, q_
         nc.vector.memset(bias_rows[:, 1, :].bitcast(F32), 0.0)
         nc.vector.memset(param_rows[:].bitcast(F32), 0.0)
         w1_blocks = w1.rearrange("(ob p) k -> p ob k", p=P)
+        nc.sync.dma_start(out=x_sb[0][:], in_=x_groups[0])
         nc.sync.dma_start(out=w1_sb[:, 0:2, :], in_=w1_blocks[:, 0:2, :])
         nc.sync.dma_start(out=w1_sb[:, 2:4, :], in_=w1_blocks[:, 2:4, :])
         for i, bias in enumerate((b1, b2)):
@@ -70,7 +70,7 @@ def tile_crossfusion_pa_t_kernel(tc, x, w1, b1, gamma, beta, w2, b2, llm_out, q_
                 out=param_rows[n * PACK : (n + 1) * PACK, :].rearrange("t (s i) -> t s i", i=RUN),
                 in_=vec.rearrange("(s t i) -> t s i", t=PACK, i=RUN),
             )
-        for g in range(GROUPS):
+        for g in range(1, GROUPS):
             if g == 4:
                 nc.sync.dma_start(out=w2_sb[:], in_=w2.rearrange("(ob p) k -> p ob k", p=P))
             nc.sync.dma_start(out=x_sb[g][:], in_=x_groups[g])
@@ -112,13 +112,17 @@ def tile_crossfusion_pa_t_kernel(tc, x, w1, b1, gamma, beta, w2, b2, llm_out, q_
         w1_grouped = const.tile([P, D, PACK], BF16, align_bytes=64)
         w1_codes = const.tile([P, D], U32, align_bytes=64)
         w1_scales = const.tile([P, D], U8, align_bytes=64)
-        def w1_half(h):
-            cols = slice(h * HALF, (h + 1) * HALF)
-            words = word_transposes(w1_sb[:, 2 * h : 2 * h + 2, :])
-            if h == 0:
-                nc.vector.tensor_copy(out=w1_grouped[:, cols, :].bitcast(F32), in_=words)
+        def w1_block(h):
+            words = w1_sb[:, h, :].bitcast(F32)
+            words_ps = psum_z.tile([P, 2, P], F32, name="w1_ps", tag="z_ps")
+            for u in range(2):
+                nc.tensor.transpose(words_ps[:, u, :], words[:, u : 2 * P : 2], ident_f32[:])
+            out = w1_grouped[:, h * P : (h + 1) * P, :].rearrange("p c t -> p (c t)").bitcast(F32)
+            out = out.rearrange("p (c u) -> p c u", u=2)
+            if h in (0, 1, 3):
+                nc.vector.tensor_copy(out=out, in_=words_ps[:].rearrange("p u c -> p c u"))
             else:
-                nc.scalar.copy(out=w1_grouped[:, cols, :].bitcast(F32), in_=words)
+                nc.scalar.copy(out=out, in_=words_ps[:].rearrange("p u c -> p c u"))
 
         def quantise_w1_half(h):
             cols = slice(h * HALF, (h + 1) * HALF)
@@ -161,44 +165,41 @@ def tile_crossfusion_pa_t_kernel(tc, x, w1, b1, gamma, beta, w2, b2, llm_out, q_
                         w2_turned[:, 2 * h + b, t * P : (t + 1) * P],
                         ident_bf[:],
                     )
-            nc.scalar.copy(
+            (nc.vector.tensor_copy if h == 1 else nc.scalar.copy)(
                 out=w2_grouped[:, h * HALF : (h + 1) * HALF, :],
                 in_=w2_ps[:].rearrange("p t c -> p c t"),
             )
 
-        grouped, codes_of, scales_of = {}, {}, {}
+        pairs, pair_codes, pair_scales = {}, {}, {}
+        halves = (slice(0, GROUP), slice(GROUP, 2 * GROUP))
         x_words, x_acc = {}, {}
         llm, sums, neg_mean, sum_sq, rstd, shift, z, z_ps = {}, {}, {}, {}, {}, {}, {}, {}
         planes, n_acc = {}, {}
+
+        def pair(a):
+            if a not in pairs:
+                pairs[a] = work.tile([P, 2 * GROUP, PACK], BF16, name="pair", align_bytes=64)
+            return pairs[a]
 
         def transpose_x(g):
             x_words[g] = word_transposes(x_sb[g][:])
 
         def copy_x(g):
-            grouped["x", g] = work.tile([P, GROUP, PACK], BF16, name="x_grouped", align_bytes=64)
-            out = grouped["x", g][:].rearrange("p c t -> p (c t)").bitcast(F32)
+            out = pair(g)[:, halves[0], :].rearrange("p c t -> p (c t)").bitcast(F32)
             out = out.rearrange("p (c u) -> p c u", u=2)
-            if g == 0:
-                nc.vector.tensor_copy(out=out, in_=x_words[g])
-            else:
-                nc.scalar.copy(out=out, in_=x_words[g])
+            nc.scalar.copy(out=out, in_=x_words[g])
 
-        def quantise_group(kind, g):
-            codes_of[kind, g] = work.tile([P, GROUP], U32, name="codes", tag=kind + "_codes", align_bytes=64)
-            scales_of[kind, g] = work.tile([P, GROUP], U8, name="scales", tag=kind + "_scales", align_bytes=64)
-            quantise(grouped[kind, g][:], codes_of[kind, g][:], scales_of[kind, g][:])
+        def quantise_pair(a):
+            cols = slice(0 if a < GROUPS else GROUP, 2 * GROUP if a >= LAG else GROUP)
+            pair_codes[a] = work.tile([P, 2 * GROUP], U32, name="pair_codes", align_bytes=64)
+            pair_scales[a] = work.tile([P, 2 * GROUP], U8, name="pair_scales", align_bytes=64)
+            quantise(pairs[a][:, cols, :], pair_codes[a][:, cols], pair_scales[a][:, cols])
 
-        def quantise_x(g):
-            quantise_group("x", g)
-
-        def quantise_n(g):
-            quantise_group("n", g)
-
-        def multiply(kind, g, w_codes, w_scales):
-            codes, scales = codes_of[kind, g], scales_of[kind, g]
+        def multiply(a, half, w_codes, w_scales):
+            codes, scales = pair_codes[a], pair_scales[a]
             accs = []
             for j in range(TILES):
-                cols = slice(j * P, (j + 1) * P)
+                cols = slice(half * GROUP + j * P, half * GROUP + (j + 1) * P)
                 acc = psum_acc.tile([P, D], F32, name="acc", tag="acc")
                 nc.tensor.matmul_mx(
                     out=acc[:],
@@ -213,7 +214,7 @@ def tile_crossfusion_pa_t_kernel(tc, x, w1, b1, gamma, beta, w2, b2, llm_out, q_
             return accs
 
         def first_matmul(g):
-            x_acc[g] = multiply("x", g, w1_codes, w1_scales)
+            x_acc[g] = multiply(g, 0, w1_codes, w1_scales)
 
         def first_bias(g):
             llm[g] = wide.tile([P, TILES, D], F32, name="llm")
@@ -234,18 +235,18 @@ def tile_crossfusion_pa_t_kernel(tc, x, w1, b1, gamma, beta, w2, b2, llm_out, q_
             neg_mean[g] = small.tile([P, TILES], F32, name="neg_mean")
             nc.scalar.mul(out=neg_mean[g][:], in_=sums[g][:], mul=-1.0 / D)
 
-        def squares(g):
-            deviations = work.tile([P, TILES, D], BF16, name="deviations")
-            sum_sq[g] = small.tile([P, TILES], F32, name="sum_sq")
-            for j in range(TILES):
-                nc.scalar.activation(
-                    out=deviations[:, j, :],
-                    in_=llm[g][:, j, :],
-                    func=ACT.Square,
-                    bias=sums[g][:, j : j + 1],
-                    scale=-float(D),
-                    accum_out=sum_sq[g][:, j : j + 1],
-                )
+        def squares(g, j):
+            if j == 0:
+                sum_sq[g] = small.tile([P, TILES], F32, name="sum_sq")
+            scaled = work.tile([P, D], BF16, name="scaled")
+            nc.scalar.activation(
+                out=scaled[:],
+                in_=llm[g][:, j, :],
+                func=ACT.Square,
+                bias=sums[g][:, j : j + 1],
+                scale=-float(D),
+                accum_out=sum_sq[g][:, j : j + 1],
+            )
 
         def inverse_deviation(g):
             rstd[g] = small.tile([P, TILES], F32, name="rstd")
@@ -308,10 +309,9 @@ def tile_crossfusion_pa_t_kernel(tc, x, w1, b1, gamma, beta, w2, b2, llm_out, q_
                 )
 
         def regroup_n(g):
-            grouped["n", g] = n_pool.tile([P, GROUP, PACK], BF16, name="n_grouped", align_bytes=64)
             columns = P if g >= 13 else GROUP
             nc.gpsimd.tensor_scalar(
-                out=grouped["n", g][:, 0:columns, :],
+                out=pair(g + LAG)[:, GROUP : GROUP + columns, :],
                 in0=planes[g][:, :, 0:columns].rearrange("p t c -> p c t"),
                 scalar1=1.0,
                 scalar2=0.0,
@@ -320,12 +320,12 @@ def tile_crossfusion_pa_t_kernel(tc, x, w1, b1, gamma, beta, w2, b2, llm_out, q_
             )
             if columns < GROUP:
                 nc.scalar.copy(
-                    out=grouped["n", g][:, columns:GROUP, :],
+                    out=pair(g + LAG)[:, GROUP + columns : 2 * GROUP, :],
                     in_=planes[g][:, :, columns:GROUP].rearrange("p t c -> p c t"),
                 )
 
         def second_matmul(g):
-            n_acc[g] = multiply("n", g, w2_codes, w2_scales)
+            n_acc[g] = multiply(g + LAG, 1, w2_codes, w2_scales)
 
         def second_bias(g):
             q = wide.tile([P, TILES, D], F32)
@@ -333,43 +333,48 @@ def tile_crossfusion_pa_t_kernel(tc, x, w1, b1, gamma, beta, w2, b2, llm_out, q_
                 nc.vector.tensor_add(out=q[:, j, :], in0=n_acc[g][j][:], in1=bias_bc[:, 1, :])
                 nc.sync.dma_start(out=q_groups[g][:, j, :], in_=q[:, j, :])
 
-        def run(stage, g):
+        def run(stage, g, *rest):
             if 0 <= g < GROUPS:
-                stage(g)
+                stage(g, *rest)
 
-        w1_half(0)
-        w1_half(1)
         transpose_x(0)
-        spread_bias(0)
-        quantise_w1_half(0)
         copy_x(0)
+        w1_block(0)
+        w1_block(1)
+        quantise_pair(0)
+        quantise_w1_half(0)
+        w1_block(2)
+        w1_block(3)
         quantise_w1_half(1)
+        spread_bias(0)
 
         for step in range(-2, GROUPS + LAG):
             run(regroup_n, step - 5)
+            run(normalise, step - 3)
             run(first_matmul, step)
             run(affine, step - 4)
             run(transpose_x, step + 3)
             if step > -2:
                 run(copy_x, step + 2)
-            run(inverse_deviation, step - 2)
-            run(normalise, step - 3)
             run(second_matmul, step - 6)
-            run(quantise_n, step - 5)
-            run(quantise_x, step + 1)
+            if 1 <= step + 1 < GROUPS + LAG:
+                quantise_pair(step + 1)
             run(transpose_z, step - 3)
             run(first_bias, step)
+            run(inverse_deviation, step - 2)
             run(mean, step - 2)
-            run(squares, step - 1)
+            run(squares, step - 1, 0)
             run(shift_of, step - 2)
+            run(squares, step - 1, 1)
             run(second_bias, step - 6)
             if step == -2:
                 turn_w2()
             if step == 1:
                 params_to_partitions()
-            if step in (2, 3):
-                w2_half(step - 2)
+            if step == 2:
+                w2_half(0)
             if step == 4:
-                quantise(w2_grouped[:], w2_codes[:], w2_scales[:])
+                w2_half(1)
             if step == 5:
                 spread_bias(1)
+                quantise(w2_grouped[:], w2_codes[:], w2_scales[:])

@@ -137,14 +137,15 @@ def tile_crossfusion_pa_t_kernel(tc, x, w1, b1, gamma, beta, w2, b2, llm_out, q_
 
         def turn_w2():
             for b in range(PACK):
-                nc.gpsimd.tensor_scalar(
-                    out=unturned(w2_turned[:, b, :]),
-                    in0=turn(w2_sb[:, b, :]),
-                    scalar1=1.0,
-                    scalar2=0.0,
-                    op0=ALU.mult,
-                    op1=ALU.add,
-                )
+                for u in range(2):
+                    nc.gpsimd.tensor_scalar(
+                        out=w2_turned[:, b, u * HALF : (u + 1) * HALF].rearrange("p (s i e) -> p s i e", i=RUN, e=2),
+                        in0=w2_sb[:, b, :].rearrange("p (s u e i) -> p u s i e", u=2, e=2, i=RUN)[:, u],
+                        scalar1=1.0,
+                        scalar2=0.0,
+                        op0=ALU.mult,
+                        op1=ALU.add,
+                    )
 
         def spread_bias(i):
             bias_ps = psum_acc.tile([P, D], F32, name="bias_ps", tag="acc")
@@ -157,17 +158,17 @@ def tile_crossfusion_pa_t_kernel(tc, x, w1, b1, gamma, beta, w2, b2, llm_out, q_
             nc.scalar.copy(out=params[:], in_=param_ps[:, 0 : 2 * PACK])
 
         def w2_half(h):
-            w2_ps = psum_acc.tile([P, PACK, HALF], BF16, name="w2_ps", tag="acc")
+            w2_ps = psum_acc.tile([P, 2, HALF], F32, name="w2_ps", tag="acc")
             for b in range(2):
-                for t in range(PACK):
+                words = w2_turned[:, 2 * h + b, :].bitcast(F32)
+                for u in range(2):
                     nc.tensor.transpose(
-                        w2_ps[:, t, b * P : (b + 1) * P],
-                        w2_turned[:, 2 * h + b, t * P : (t + 1) * P],
-                        ident_bf[:],
+                        w2_ps[:, u, b * P : (b + 1) * P], words[:, u * P : (u + 1) * P], ident_f32[:]
                     )
+            out = w2_grouped[:, h * HALF : (h + 1) * HALF, :].rearrange("p c t -> p (c t)").bitcast(F32)
             (nc.vector.tensor_copy if h == 1 else nc.scalar.copy)(
-                out=w2_grouped[:, h * HALF : (h + 1) * HALF, :],
-                in_=w2_ps[:].rearrange("p t c -> p c t"),
+                out=out.rearrange("p (c u) -> p c u", u=2),
+                in_=w2_ps[:].rearrange("p u c -> p c u"),
             )
 
         pairs, pair_codes, pair_scales = {}, {}, {}
@@ -255,7 +256,7 @@ def tile_crossfusion_pa_t_kernel(tc, x, w1, b1, gamma, beta, w2, b2, llm_out, q_
             )
 
         def on_scalar(g, j):
-            return j == 1 and g % 4 != 3 and 4 <= g < 14
+            return j == 1 and g % 2 == 0 and 4 <= g < 14
 
         def shift_of(g):
             if on_scalar(g, 1):
@@ -267,7 +268,16 @@ def tile_crossfusion_pa_t_kernel(tc, x, w1, b1, gamma, beta, w2, b2, llm_out, q_
         def normalise(g):
             z[g] = work.tile([P, TILES, D], F32, name="z")
             for j in range(TILES):
-                if on_scalar(g, j):
+                if j == 1 and g % 2 == 1 and g < 14:
+                    nc.gpsimd.tensor_scalar(
+                        out=unturned(z[g][:, j, :]),
+                        in0=turn(llm[g][:, j, :]),
+                        scalar1=neg_mean[g][:, j : j + 1],
+                        scalar2=rstd[g][:, j : j + 1],
+                        op0=ALU.add,
+                        op1=ALU.mult,
+                    )
+                elif on_scalar(g, j):
                     nc.scalar.activation(
                         out=unturned(z[g][:, j, :]),
                         in_=turn(llm[g][:, j, :]),

@@ -41,8 +41,8 @@ def tile_crossfusion_pa_t_kernel(tc, x, w1, b1, gamma, beta, w2, b2, llm_out, q_
         wide = stack.enter_context(tc.tile_pool(name="wide", bufs=7))
         small = stack.enter_context(tc.tile_pool(name="small", bufs=7))
         psum_t = stack.enter_context(tc.psum_pool(name="psum_t", bufs=2))
-        psum_acc = stack.enter_context(tc.psum_pool(name="psum_acc", bufs=3))
-        psum_z = stack.enter_context(tc.psum_pool(name="psum_z", bufs=3))
+        psum_acc = stack.enter_context(tc.psum_pool(name="psum_acc", bufs=4))
+        psum_z = stack.enter_context(tc.psum_pool(name="psum_z", bufs=2))
 
         x_sb = []
         for g in range(GROUPS):
@@ -150,7 +150,7 @@ def tile_crossfusion_pa_t_kernel(tc, x, w1, b1, gamma, beta, w2, b2, llm_out, q_
         def spread_bias(i):
             bias_ps = psum_acc.tile([P, D], F32, name="bias_ps", tag="acc")
             nc.tensor.matmul(bias_ps[:], lhsT=ones[:], rhs=bias_rows[:, i, :], start=True, stop=True)
-            nc.scalar.copy(out=bias_bc[:, i, :], in_=bias_ps[:])
+            (nc.scalar.copy if i == 0 else nc.vector.tensor_copy)(out=bias_bc[:, i, :], in_=bias_ps[:])
 
         def params_to_partitions():
             param_ps = psum_t.tile([P, P], BF16, name="param_ps", tag="tp")
@@ -258,6 +258,11 @@ def tile_crossfusion_pa_t_kernel(tc, x, w1, b1, gamma, beta, w2, b2, llm_out, q_
         def on_scalar(g, j):
             return j == 1 and g % 2 == 0 and 4 <= g < 14
 
+        def on_gpsimd(g, j):
+            if 4 <= g < 14:
+                return j == g % 2
+            return j == 1 and g == 1
+
         def shift_of(g):
             if on_scalar(g, 1):
                 shift[g] = small.tile([P, 1], F32, name="shift")
@@ -268,7 +273,7 @@ def tile_crossfusion_pa_t_kernel(tc, x, w1, b1, gamma, beta, w2, b2, llm_out, q_
         def normalise(g):
             z[g] = work.tile([P, TILES, D], F32, name="z")
             for j in range(TILES):
-                if j == 1 and g % 2 == 1 and g < 14:
+                if on_gpsimd(g, j):
                     nc.gpsimd.tensor_scalar(
                         out=unturned(z[g][:, j, :]),
                         in0=turn(llm[g][:, j, :]),
@@ -319,7 +324,7 @@ def tile_crossfusion_pa_t_kernel(tc, x, w1, b1, gamma, beta, w2, b2, llm_out, q_
                 )
 
         def regroup_n(g):
-            columns = P if g >= 13 else GROUP
+            columns = P if g >= 13 else GROUP - 32 if g >= 8 else GROUP
             nc.gpsimd.tensor_scalar(
                 out=pair(g + LAG)[:, GROUP : GROUP + columns, :],
                 in0=planes[g][:, :, 0:columns].rearrange("p t c -> p c t"),
@@ -377,14 +382,12 @@ def tile_crossfusion_pa_t_kernel(tc, x, w1, b1, gamma, beta, w2, b2, llm_out, q_
             run(shift_of, step - 2)
             run(squares, step - 1, 1)
             run(second_bias, step - 6)
-            if step == -2:
+            if step == 0:
                 turn_w2()
-            if step == 1:
                 params_to_partitions()
-            if step == 2:
-                w2_half(0)
+            if step in (2, 3):
+                w2_half(step - 2)
             if step == 4:
-                w2_half(1)
+                quantise(w2_grouped[:], w2_codes[:], w2_scales[:])
             if step == 5:
                 spread_bias(1)
-                quantise(w2_grouped[:], w2_codes[:], w2_scales[:])

from contextlib import ExitStack

import concourse.mybir as mybir
from concourse.masks import make_identity

F32 = mybir.dt.float32
BF16 = mybir.dt.bfloat16
U32 = mybir.dt.uint32
U8 = mybir.dt.uint8
FP8X4 = mybir.dt.float8_e4m3fn_x4
ACT = mybir.ActivationFunctionType
ALU = mybir.AluOpType

P = 128
PACK = 4
D = P * PACK
TOKENS = 16 * 256
TILES = 2
GROUP = P * TILES
GROUPS = TOKENS // GROUP
LAG = 6
HALF = D // 2
RUN = 8
WARM_UP = 3
EPS = 1e-5

FLOPS = 2 * 2 * TOKENS * D * D


def tile_crossfusion_pa_t_kernel(tc, x, w1, b1, gamma, beta, w2, b2, llm_out, q_out):
    nc = tc.nc
    x_groups = x.flatten_outer_dims().rearrange("(g p j) k -> g p j k", p=P, j=TILES)
    llm_groups = llm_out.flatten_outer_dims().rearrange("(g p j) f -> g p j f", p=P, j=TILES)
    q_groups = q_out.flatten_outer_dims().rearrange("(g p j) f -> g p j f", p=P, j=TILES)

    with ExitStack() as stack:
        stack.enter_context(tc.manual_schedule())
        const = stack.enter_context(tc.tile_pool(name="const", bufs=1))
        x_pool = stack.enter_context(tc.tile_pool(name="x_pool", bufs=GROUPS))
        work = stack.enter_context(tc.tile_pool(name="work", bufs=4))
        wide = stack.enter_context(tc.tile_pool(name="wide", bufs=7))
        small = stack.enter_context(tc.tile_pool(name="small", bufs=7))
        psum_t = stack.enter_context(tc.psum_pool(name="psum_t", bufs=2))
        psum_acc = stack.enter_context(tc.psum_pool(name="psum_acc", bufs=4))
        psum_z = stack.enter_context(tc.psum_pool(name="psum_z", bufs=2))

        x_sb = []
        for g in range(GROUPS):
            x_sb.append(x_pool.tile([P, TILES, D], BF16, name="x_sb", tag="x_sb"))
        w1_sb = const.tile([P, PACK, D], BF16)
        w2_sb = const.tile([P, PACK, D], BF16)
        bias_rows = const.tile([P, 2, D], BF16)
        param_rows = const.tile([P, P], BF16)
        warm = const.tile([P, 1], F32)
        nc.vector.memset(warm[:], 1.0)
        nc.scalar.activation(out=warm[:], in_=warm[:], func=ACT.Abs_reciprocal_sqrt)
        idle_rows = const.tile([P, D], BF16)
        nc.vector.memset(idle_rows[:].bitcast(F32), 0.0)
        nc.vector.memset(bias_rows[:, 0, :].bitcast(F32), 0.0)
        nc.vector.memset(bias_rows[:, 1, :].bitcast(F32), 0.0)
        nc.vector.memset(param_rows[:].bitcast(F32), 0.0)
        w1_blocks = w1.rearrange("(ob p) k -> p ob k", p=P)
        nc.sync.dma_start(out=x_sb[0][:], in_=x_groups[0])
        nc.sync.dma_start(out=w1_sb[:, 0:2, :], in_=w1_blocks[:, 0:2, :])
        nc.sync.dma_start(out=w1_sb[:, 2:4, :], in_=w1_blocks[:, 2:4, :])
        for i, bias in enumerate((b1, b2)):
            nc.scalar.dma_start(out=bias_rows[0:1, i, :], in_=bias.rearrange("(o f) -> o f", o=1))
        for n, vec in enumerate((gamma, beta)):
            nc.scalar.dma_start(
                out=param_rows[n * PACK : (n + 1) * PACK, :].rearrange("t (s i) -> t s i", i=RUN),
                in_=vec.rearrange("(s t i) -> t s i", t=PACK, i=RUN),
            )
        for g in range(1, GROUPS):
            if g == 4:
                nc.sync.dma_start(out=w2_sb[:], in_=w2.rearrange("(ob p) k -> p ob k", p=P))
            nc.sync.dma_start(out=x_sb[g][:], in_=x_groups[g])

        ident_f32 = const.tile([P, P], F32)
        make_identity(nc, ident_f32[:])
        ident_bf = const.tile([P, P], BF16)
        make_identity(nc, ident_bf[:])
        ones = const.tile([P, P], BF16)
        nc.vector.memset(ones[:], 1.0)

        def word_transposes(rows):
            words = rows.bitcast(F32)
            words_ps = psum_t.tile([P, 2, 2 * P], F32, name="words_ps", tag="tp")
            for b in range(2):
                for u in range(2):
                    nc.tensor.transpose(
                        words_ps[:, u, b * P : (b + 1) * P], words[:, b, u : 2 * P : 2], ident_f32[:]
                    )
            return words_ps[:].rearrange("p u c -> p c u")

        def quantise(grouped, codes, scales):
            nc.vector.quantize_mx(
                out=codes.bitcast(FP8X4),
                scales=scales,
                in_=grouped.rearrange("p c t -> p (c t)"),
            )

        def turn(features):
            return features.rearrange("p (s t i) -> p t s i", t=PACK, i=RUN)

        def unturned(features):
            return features.rearrange("p (t s i) -> p t s i", t=PACK, i=RUN)

        idle_ps = psum_acc.tile([P, D], F32, name="idle_ps", tag="acc")
        for n in range(WARM_UP):
            nc.tensor.matmul(idle_ps[:], lhsT=idle_rows[:, 0:P], rhs=idle_rows[:], start=True, stop=True)

        w1_grouped = const.tile([P, D, PACK], BF16, align_bytes=64)
        w1_codes = const.tile([P, D], U32, align_bytes=64)
        w1_scales = const.tile([P, D], U8, align_bytes=64)
        def w1_block(h):
            words = w1_sb[:, h, :].bitcast(F32)
            words_ps = psum_z.tile([P, 2, P], F32, name="w1_ps", tag="z_ps")
            for u in range(2):
                nc.tensor.transpose(words_ps[:, u, :], words[:, u : 2 * P : 2], ident_f32[:])
            out = w1_grouped[:, h * P : (h + 1) * P, :].rearrange("p c t -> p (c t)").bitcast(F32)
            out = out.rearrange("p (c u) -> p c u", u=2)
            if h in (0, 1, 3):
                nc.vector.tensor_copy(out=out, in_=words_ps[:].rearrange("p u c -> p c u"))
            else:
                nc.scalar.copy(out=out, in_=words_ps[:].rearrange("p u c -> p c u"))

        def quantise_w1_half(h):
            cols = slice(h * HALF, (h + 1) * HALF)
            quantise(w1_grouped[:, cols, :], w1_codes[:, cols], w1_scales[:, cols])

        bias_bc = const.tile([P, 2, D], F32)
        params = const.tile([P, 2 * PACK], F32)
        w2_turned = const.tile([P, PACK, D], BF16)
        w2_grouped = const.tile([P, D, PACK], BF16, align_bytes=64)
        w2_codes = const.tile([P, D], U32, align_bytes=64)
        w2_scales = const.tile([P, D], U8, align_bytes=64)

        def turn_w2():
            for b in range(PACK):
                for u in range(2):
                    nc.gpsimd.tensor_scalar(
                        out=w2_turned[:, b, u * HALF : (u + 1) * HALF].rearrange("p (s i e) -> p s i e", i=RUN, e=2),
                        in0=w2_sb[:, b, :].rearrange("p (s u e i) -> p u s i e", u=2, e=2, i=RUN)[:, u],
                        scalar1=1.0,
                        scalar2=0.0,
                        op0=ALU.mult,
                        op1=ALU.add,
                    )

        def spread_bias(i):
            bias_ps = psum_acc.tile([P, D], F32, name="bias_ps", tag="acc")
            nc.tensor.matmul(bias_ps[:], lhsT=ones[:], rhs=bias_rows[:, i, :], start=True, stop=True)
            (nc.scalar.copy if i == 0 else nc.vector.tensor_copy)(out=bias_bc[:, i, :], in_=bias_ps[:])

        def params_to_partitions():
            param_ps = psum_t.tile([P, P], BF16, name="param_ps", tag="tp")
            nc.tensor.transpose(param_ps[:], param_rows[:], ident_bf[:])
            nc.scalar.copy(out=params[:], in_=param_ps[:, 0 : 2 * PACK])

        def w2_half(h):
            w2_ps = psum_acc.tile([P, 2, HALF], F32, name="w2_ps", tag="acc")
            for b in range(2):
                words = w2_turned[:, 2 * h + b, :].bitcast(F32)
                for u in range(2):
                    nc.tensor.transpose(
                        w2_ps[:, u, b * P : (b + 1) * P], words[:, u * P : (u + 1) * P], ident_f32[:]
                    )
            out = w2_grouped[:, h * HALF : (h + 1) * HALF, :].rearrange("p c t -> p (c t)").bitcast(F32)
            (nc.vector.tensor_copy if h == 1 else nc.scalar.copy)(
                out=out.rearrange("p (c u) -> p c u", u=2),
                in_=w2_ps[:].rearrange("p u c -> p c u"),
            )

        pairs, pair_codes, pair_scales = {}, {}, {}
        halves = (slice(0, GROUP), slice(GROUP, 2 * GROUP))
        x_words, x_acc = {}, {}
        llm, sums, neg_mean, sum_sq, rstd, shift, z, z_ps = {}, {}, {}, {}, {}, {}, {}, {}
        planes, n_acc = {}, {}

        def pair(a):
            if a not in pairs:
                pairs[a] = work.tile([P, 2 * GROUP, PACK], BF16, name="pair", align_bytes=64)
            return pairs[a]

        def transpose_x(g):
            x_words[g] = word_transposes(x_sb[g][:])

        def copy_x(g):
            out = pair(g)[:, halves[0], :].rearrange("p c t -> p (c t)").bitcast(F32)
            out = out.rearrange("p (c u) -> p c u", u=2)
            nc.scalar.copy(out=out, in_=x_words[g])

        def quantise_pair(a):
            cols = slice(0 if a < GROUPS else GROUP, 2 * GROUP if a >= LAG else GROUP)
            pair_codes[a] = work.tile([P, 2 * GROUP], U32, name="pair_codes", align_bytes=64)
            pair_scales[a] = work.tile([P, 2 * GROUP], U8, name="pair_scales", align_bytes=64)
            quantise(pairs[a][:, cols, :], pair_codes[a][:, cols], pair_scales[a][:, cols])

        def multiply(a, half, w_codes, w_scales):
            codes, scales = pair_codes[a], pair_scales[a]
            accs = []
            for j in range(TILES):
                cols = slice(half * GROUP + j * P, half * GROUP + (j + 1) * P)
                acc = psum_acc.tile([P, D], F32, name="acc", tag="acc")
                nc.tensor.matmul_mx(
                    out=acc[:],
                    lhsT=codes[:, cols].bitcast(FP8X4),
                    lhsT_scale=scales[:, cols],
                    rhs=w_codes[:].bitcast(FP8X4),
                    rhs_scale=w_scales[:],
                    start=True,
                    stop=True,
                )
                accs.append(acc)
            return accs

        def first_matmul(g):
            x_acc[g] = multiply(g, 0, w1_codes, w1_scales)

        def first_bias(g):
            llm[g] = wide.tile([P, TILES, D], F32, name="llm")
            sums[g] = small.tile([P, TILES], F32, name="sums")
            for j in range(TILES):
                nc.vector.scalar_tensor_tensor(
                    out=llm[g][:, j, :],
                    in0=x_acc[g][j][:],
                    scalar=1.0,
                    in1=bias_bc[:, 0, :],
                    op0=ALU.mult,
                    op1=ALU.add,
                    accum_out=sums[g][:, j : j + 1],
                )
            nc.sync.dma_start(out=llm_groups[g], in_=llm[g][:])

        def mean(g):
            neg_mean[g] = small.tile([P, TILES], F32, name="neg_mean")
            nc.scalar.mul(out=neg_mean[g][:], in_=sums[g][:], mul=-1.0 / D)

        def squares(g, j):
            if j == 0:
                sum_sq[g] = small.tile([P, TILES], F32, name="sum_sq")
            scaled = work.tile([P, D], BF16, name="scaled")
            nc.scalar.activation(
                out=scaled[:],
                in_=llm[g][:, j, :],
                func=ACT.Square,
                bias=sums[g][:, j : j + 1],
                scale=-float(D),
                accum_out=sum_sq[g][:, j : j + 1],
            )

        def inverse_deviation(g):
            rstd[g] = small.tile([P, TILES], F32, name="rstd")
            nc.scalar.activation(
                out=rstd[g][:], in_=sum_sq[g][:], func=ACT.Abs_reciprocal_sqrt, bias=EPS, scale=1.0 / D**3
            )

        def on_scalar(g, j):
            return j == 1 and g % 2 == 0 and 4 <= g < 14

        def on_gpsimd(g, j):
            if 4 <= g < 14:
                return j == g % 2
            return j == 1 and g == 1

        def shift_of(g):
            if on_scalar(g, 1):
                shift[g] = small.tile([P, 1], F32, name="shift")
                nc.scalar.activation(
                    out=shift[g][:], in_=neg_mean[g][:, 1:2], func=ACT.Identity, scale=rstd[g][:, 1:2]
                )

        def normalise(g):
            z[g] = work.tile([P, TILES, D], F32, name="z")
            for j in range(TILES):
                if on_gpsimd(g, j):
                    nc.gpsimd.tensor_scalar(
                        out=unturned(z[g][:, j, :]),
                        in0=turn(llm[g][:, j, :]),
                        scalar1=neg_mean[g][:, j : j + 1],
                        scalar2=rstd[g][:, j : j + 1],
                        op0=ALU.add,
                        op1=ALU.mult,
                    )
                elif on_scalar(g, j):
                    nc.scalar.activation(
                        out=unturned(z[g][:, j, :]),
                        in_=turn(llm[g][:, j, :]),
                        func=ACT.Identity,
                        bias=shift[g][:],
                        scale=rstd[g][:, j : j + 1],
                    )
                else:
                    nc.vector.tensor_scalar(
                        out=unturned(z[g][:, j, :]),
                        in0=turn(llm[g][:, j, :]),
                        scalar1=neg_mean[g][:, j : j + 1],
                        scalar2=rstd[g][:, j : j + 1],
                        op0=ALU.add,
                        op1=ALU.mult,
                    )

        def transpose_z(g):
            z_ps[g] = []
            for h in range(2):
                half = psum_z.tile([P, 2, GROUP], F32, name="z_ps", tag="z_ps")
                for i in range(2):
                    t = 2 * h + i
                    for j in range(TILES):
                        nc.tensor.transpose(
                            half[:, i, j * P : (j + 1) * P], z[g][:, j, t * P : (t + 1) * P], ident_f32[:]
                        )
                z_ps[g].append(half)

        def affine(g):
            planes[g] = work.tile([P, PACK, GROUP], BF16, name="planes")
            for t in range(PACK):
                nc.scalar.activation(
                    out=planes[g][:, t, :],
                    in_=z_ps[g][t // 2][:, t % 2, :],
                    func=ACT.Identity,
                    bias=params[:, PACK + t : PACK + t + 1],
                    scale=params[:, t : t + 1],
                )

        def regroup_n(g):
            columns = P if g >= 13 else GROUP - 32 if g >= 8 else GROUP
            nc.gpsimd.tensor_scalar(
                out=pair(g + LAG)[:, GROUP : GROUP + columns, :],
                in0=planes[g][:, :, 0:columns].rearrange("p t c -> p c t"),
                scalar1=1.0,
                scalar2=0.0,
                op0=ALU.mult,
                op1=ALU.add,
            )
            if columns < GROUP:
                nc.scalar.copy(
                    out=pair(g + LAG)[:, GROUP + columns : 2 * GROUP, :],
                    in_=planes[g][:, :, columns:GROUP].rearrange("p t c -> p c t"),
                )

        def second_matmul(g):
            n_acc[g] = multiply(g + LAG, 1, w2_codes, w2_scales)

        def second_bias(g):
            q = wide.tile([P, TILES, D], F32)
            for j in range(TILES):
                nc.vector.tensor_add(out=q[:, j, :], in0=n_acc[g][j][:], in1=bias_bc[:, 1, :])
                nc.sync.dma_start(out=q_groups[g][:, j, :], in_=q[:, j, :])

        def run(stage, g, *rest):
            if 0 <= g < GROUPS:
                stage(g, *rest)

        transpose_x(0)
        copy_x(0)
        w1_block(0)
        w1_block(1)
        quantise_pair(0)
        quantise_w1_half(0)
        w1_block(2)
        w1_block(3)
        quantise_w1_half(1)
        spread_bias(0)

        for step in range(-2, GROUPS + LAG):
            run(regroup_n, step - 5)
            run(normalise, step - 3)
            run(first_matmul, step)
            run(affine, step - 4)
            run(transpose_x, step + 3)
            if step > -2:
                run(copy_x, step + 2)
            run(second_matmul, step - 6)
            if 1 <= step + 1 < GROUPS + LAG:
                quantise_pair(step + 1)
            run(transpose_z, step - 3)
            run(first_bias, step)
            run(inverse_deviation, step - 2)
            run(mean, step - 2)
            run(squares, step - 1, 0)
            run(shift_of, step - 2)
            run(squares, step - 1, 1)
            run(second_bias, step - 6)
            if step == 0:
                turn_w2()
                params_to_partitions()
            if step in (2, 3):
                w2_half(step - 2)
            if step == 4:
                quantise(w2_grouped[:], w2_codes[:], w2_scales[:])
            if step == 5:
                spread_bias(1)
